import numpy as np
import ml_dtypes


def mxq(x, axis, fmt="e4m3"):
    dtype, down = {"e4m3": (ml_dtypes.float8_e4m3fn, 7), "e5m2": (ml_dtypes.float8_e5m2, 14)}[fmt]
    v = np.moveaxis(np.asarray(x, np.float32).astype(ml_dtypes.bfloat16).astype(np.float64), axis, -1)
    blocks = v.reshape(v.shape[:-1] + (-1, 32))
    amax = np.abs(blocks).max(-1, keepdims=True)
    byte = np.maximum(np.where(amax > 0, np.frexp(amax)[1] - 1 + 127, 0) - down, 1)
    scale = np.exp2(byte - 127.0)
    codes = (blocks / scale).astype(np.float32).astype(dtype).astype(np.float64)
    return np.moveaxis((codes * scale).reshape(v.shape), -1, axis)


WIDE = False


def mx_kscale(k):
    if not WIDE:
        return np.ones(k)
    levels = np.array([10, -10, 5, -5, 0])
    if k % 512:
        return np.exp2(np.random.permutation(np.resize(levels, k // 32))).repeat(32)
    a = np.empty((k // 512, 16))
    for p in range(k // 512):
        a[p, :8] = np.random.permutation(np.resize(levels, 8))
        for g in range(8):
            far = levels[np.abs(levels - a[p, g]) >= 10]
            a[p, g + 8] = far[np.random.randint(len(far))]
    return np.exp2(a.ravel()).repeat(32)


BF16 = ml_dtypes.bfloat16


def bf(x):
    return np.asarray(x, np.float32).astype(BF16)


def f64(x):
    return np.asarray(x).astype(np.float64)


B, S, D, NH = 2, 512, 1024, 8
SCALE = np.sqrt(D // NH)


def setup_inputs():
    s, t = mx_kscale(D), mx_kscale(D)
    return {"x": bf(np.random.standard_normal((B, S, D)) * s),
            "wq": bf(np.random.standard_normal((D, D)) * 0.84 / np.sqrt(D) / s[None, :] * t[:, None]),
            "wk": bf(np.random.standard_normal((D, D)) * 0.84 / np.sqrt(D) / s[None, :] / t[:, None])}


def reference(x, wq, wk):
    xq = mxq(f64(x), 2, "e4m3")
    q = xq @ mxq(f64(wq), 1, "e4m3").T
    k = xq @ mxq(f64(wk), 1, "e4m3").T
    sc = (mxq(q, 2, "e4m3") @ mxq(k, 2, "e4m3").transpose(0, 2, 1)) / SCALE
    e = np.exp(sc - sc.max(-1, keepdims=True))
    return e / e.sum(-1, keepdims=True)

@@ -1,0 +1,257 @@
+from contextlib import ExitStack
+import math
+
+import concourse.mybir as mybir
+from concourse.masks import make_identity
+
+F32 = mybir.dt.float32
+BF16 = mybir.dt.bfloat16
+U32 = mybir.dt.uint32
+U8 = mybir.dt.uint8
+FP8X4 = mybir.dt.float8_e4m3fn_x4
+EXP = mybir.ActivationFunctionType.Exp
+
+P = 128
+PACK = 4
+K_PASS = P * PACK
+B, S, D = 2, 512, 1024
+PASSES = D // K_PASS
+TILES = S // P
+WORDS = D // 2
+INV_SQRT = 1.0 / math.sqrt(D // 8)
+WARM_UP = 6
+
+FLOPS = 2 * (2 * B * S * D * D) + 2 * B * S * S * D
+
+
+def tile_attentionnet_pa_kernel(tc, x, wq, wk, out):
+    nc = tc.nc
+    with ExitStack() as ctx:
+        keep = ctx.enter_context(tc.tile_pool(name="keep", bufs=1))
+        stage = ctx.enter_context(tc.tile_pool(name="stage", bufs=4))
+        small = ctx.enter_context(tc.tile_pool(name="small", bufs=4))
+        work = ctx.enter_context(tc.psum_pool(name="work", bufs=6))
+        score_pool = ctx.enter_context(tc.psum_pool(name="score_pool", bufs=2))
+        ctx.enter_context(tc.manual_schedule())
+
+        identity = keep.tile([P, P], F32, name="identity")
+        make_identity(nc, identity[:])
+        zero = keep.tile([P, 1], F32, name="zero")
+        one = keep.tile([P, 1], F32, name="one")
+        nc.vector.memset(zero[:], 0.0)
+        nc.scalar.activation(out=one[:], in_=zero[:], func=EXP)
+
+        zeros = keep.tile([P, S], BF16, name="zeros")
+        nc.vector.memset(zeros[:], 0.0)
+
+        def keep_tensor_engine_busy(count):
+            for n in range(count):
+                unread = work.tile([P, S], F32, tag="work")
+                nc.tensor.matmul(
+                    out=unread[:], lhsT=zeros[:, :P], rhs=zeros[:], start=True, stop=True
+                )
+
+        def chunk_of_weights(w, g):
+            return w.rearrange("(g p j) k -> g p j k", p=P, j=PACK)[g]
+
+        def chunk_of_tokens(b):
+            return x[b].rearrange("(i p) k -> p i k", p=P)
+
+        sources = {
+            "k0": chunk_of_weights(wk, 0),
+            "x0": chunk_of_tokens(0),
+            "k1": chunk_of_weights(wk, 1),
+            "q0": chunk_of_weights(wq, 0),
+            "q1": chunk_of_weights(wq, 1),
+            "x1": chunk_of_tokens(1),
+        }
+        raw = {}
+        in_codes = {}
+        in_scales = {}
+        for name, source in sources.items():
+            raw[name] = keep.tile([P, TILES * D], BF16, name="raw_" + name)
+            in_codes[name] = keep.tile(
+                [P, TILES * PASSES * P], U32, name="codes_" + name, align_bytes=64
+            )
+            in_scales[name] = keep.tile(
+                [P, TILES * PASSES * P], U8, name="scales_" + name, align_bytes=64
+            )
+            rows = raw[name][:].rearrange("p (r k) -> p r k", r=TILES)
+            if name in ("k0", "x0"):
+                for r in range(TILES):
+                    nc.sync.dma_start(out=rows[:, r, :], in_=source[:, r, :])
+            else:
+                nc.sync.dma_start(out=rows, in_=source)
+
+        def block(codes_or_scales, r, c):
+            first = (r * PASSES + c) * P
+            return codes_or_scales[:, first : first + P]
+
+        def empty_bank(n, dst, src):
+            if n % 4 == 1:
+                nc.vector.tensor_copy(out=dst, in_=src)
+            else:
+                nc.scalar.copy(out=dst, in_=src)
+
+        def transpose_chunk(name, loads_set_the_pace=False):
+            words = raw[name][:].bitcast(F32)
+            grouped = {}
+
+            def quantise(r):
+                first = r * PASSES * P
+                nc.vector.quantize_mx(
+                    out=in_codes[name][:, first : first + PASSES * P].bitcast(FP8X4),
+                    scales=in_scales[name][:, first : first + PASSES * P],
+                    in_=grouped[r][:],
+                )
+
+            for r in range(TILES):
+                bank = work.tile([P, PASSES, 2, P], F32, tag="work")
+                for c in range(PASSES):
+                    for u in range(2):
+                        first = r * WORDS + 2 * c * P
+                        nc.tensor.transpose(
+                            bank[:, c, u, :],
+                            words[:, first + u : first + 2 * P : 2],
+                            identity[:],
+                        )
+                if loads_set_the_pace:
+                    keep_tensor_engine_busy(1)
+                grouped[r] = stage.tile(
+                    [P, PASSES * P * PACK],
+                    BF16,
+                    name="grouped_in",
+                    tag="grouped_in",
+                    align_bytes=64,
+                )
+                empty_bank(
+                    r,
+                    grouped[r][:]
+                    .bitcast(F32)
+                    .rearrange("p (c r u) -> p c r u", c=PASSES, u=2),
+                    bank[:].rearrange("p c u r -> p c r u"),
+                )
+                if r > 0:
+                    quantise(r - 1)
+            quantise(TILES - 1)
+
+        qk_codes = {}
+        qk_scales = {}
+        for name in ("q", "k"):
+            for b in range(B):
+                qk_codes[name, b] = keep.tile(
+                    [P, PASSES * S], U32, name="proj_codes_%s%d" % (name, b), align_bytes=64
+                )
+                qk_scales[name, b] = keep.tile(
+                    [P, PASSES * S], U8, name="proj_scales_%s%d" % (name, b), align_bytes=64
+                )
+
+        def project_pair(name, b, pair, n):
+            xb = "x%d" % b
+            grouped = {}
+            for m, (g, i) in enumerate(pair):
+                w = "%s%d" % (name, g)
+                bank = work.tile([P, PACK, P], F32, tag="work")
+                for t in range(PACK):
+                    for c in range(PASSES):
+                        nc.tensor.matmul_mx(
+                            out=bank[:, t, :],
+                            lhsT=block(in_codes[w], t, c).bitcast(FP8X4),
+                            lhsT_scale=block(in_scales[w], t, c),
+                            rhs=block(in_codes[xb], i, c).bitcast(FP8X4),
+                            rhs_scale=block(in_scales[xb], i, c),
+                            start=(c == 0),
+                            stop=(c == PASSES - 1),
+                        )
+                grouped[m] = stage.tile(
+                    [P, P * PACK], BF16, name="grouped_qk", tag="grouped_qk", align_bytes=64
+                )
+                empty_bank(
+                    n + m,
+                    grouped[m][:].rearrange("p (r t) -> p r t", t=PACK),
+                    bank[:].rearrange("p t r -> p r t"),
+                )
+            for m, (g, i) in enumerate(pair):
+                first = g * S + i * P
+                nc.vector.quantize_mx(
+                    out=qk_codes[name, b][:, first : first + P].bitcast(FP8X4),
+                    scales=qk_scales[name, b][:, first : first + P],
+                    in_=grouped[m][:],
+                )
+
+        def project_keys(g, b):
+            project_pair("k", b, [(g, 0), (g, 1)], 0)
+            project_pair("k", b, [(g, 2), (g, 3)], 2)
+
+        def project_queries(b, i):
+            project_pair("q", b, [(0, i), (1, i)], 2 * (i % 2))
+
+        score = {}
+        shift = {}
+        weights = {}
+        row_sum = {}
+
+        def scores_and_max(b, i):
+            score[b, i] = score_pool.tile([P, S], F32, name="score", tag="score")
+            for g in range(PASSES):
+                first = g * S + i * P
+                nc.tensor.matmul_mx(
+                    out=score[b, i][:],
+                    lhsT=qk_codes["q", b][:, first : first + P].bitcast(FP8X4),
+                    lhsT_scale=qk_scales["q", b][:, first : first + P],
+                    rhs=qk_codes["k", b][:, g * S : (g + 1) * S].bitcast(FP8X4),
+                    rhs_scale=qk_scales["k", b][:, g * S : (g + 1) * S],
+                    start=(g == 0),
+                    stop=(g == PASSES - 1),
+                )
+            row_max = small.tile([P, 1], F32, tag="row_max")
+            nc.vector.reduce_max(
+                out=row_max[:], in_=score[b, i][:], axis=mybir.AxisListType.X
+            )
+            shift[b, i] = small.tile([P, 1], F32, name="shift", tag="shift")
+            nc.vector.tensor_scalar_mul(
+                out=shift[b, i][:], in0=row_max[:], scalar1=-INV_SQRT
+            )
+
+        def exponentials(b, i):
+            weights[b, i] = stage.tile([P, S], F32, name="weights", tag="weights")
+            row_sum[b, i] = small.tile([P, 1], F32, name="row_sum", tag="row_sum")
+            nc.scalar.activation(
+                out=weights[b, i][:],
+                in_=score[b, i][:],
+                func=EXP,
+                bias=shift[b, i][:],
+                scale=INV_SQRT,
+                accum_out=row_sum[b, i][:],
+            )
+
+        def normalise_and_store(b, i):
+            inverse = small.tile([P, 1], F32, tag="inverse")
+            nc.vector.reciprocal(out=inverse[:], in_=row_sum[b, i][:])
+            nc.vector.tensor_scalar_mul(
+                out=weights[b, i][:], in0=weights[b, i][:], scalar1=inverse[:]
+            )
+            nc.sync.dma_start(out=out[b, i * P : (i + 1) * P, :], in_=weights[b, i][:])
+
+        keep_tensor_engine_busy(WARM_UP)
+        transpose_chunk("k0", loads_set_the_pace=True)
+        transpose_chunk("x0", loads_set_the_pace=True)
+        project_keys(0, 0)
+        transpose_chunk("k1")
+        transpose_chunk("q0")
+        project_keys(1, 0)
+        transpose_chunk("q1")
+        transpose_chunk("x1")
+        tiles = [(b, i) for b in range(B) for i in range(TILES)]
+        for n in range(len(tiles) + 2):
+            if n < len(tiles):
+                b, i = tiles[n]
+                if b > 0 and i == 0:
+                    project_keys(0, b)
+                    project_keys(1, b)
+                project_queries(b, i)
+            if 1 <= n <= len(tiles):
+                scores_and_max(*tiles[n - 1])
+            if n >= 2:
+                exponentials(*tiles[n - 2])
+                normalise_and_store(*tiles[n - 2])

@@ -28,10 +28,10 @@ def tile_attentionnet_pa_kernel(tc, x, wq, wk, out):
     nc = tc.nc
     with ExitStack() as ctx:
         keep = ctx.enter_context(tc.tile_pool(name="keep", bufs=1))
-        stage = ctx.enter_context(tc.tile_pool(name="stage", bufs=4))
+        stage = ctx.enter_context(tc.tile_pool(name="stage", bufs=6))
         small = ctx.enter_context(tc.tile_pool(name="small", bufs=4))
-        work = ctx.enter_context(tc.psum_pool(name="work", bufs=6))
-        score_pool = ctx.enter_context(tc.psum_pool(name="score_pool", bufs=2))
+        work = ctx.enter_context(tc.psum_pool(name="work", bufs=5))
+        score_pool = ctx.enter_context(tc.psum_pool(name="score_pool", bufs=3))
         ctx.enter_context(tc.manual_schedule())
 
         identity = keep.tile([P, P], F32, name="identity")
@@ -58,17 +58,17 @@ def tile_attentionnet_pa_kernel(tc, x, wq, wk, out):
             return x[b].rearrange("(i p) k -> p i k", p=P)
 
         sources = {
-            "k0": chunk_of_weights(wk, 0),
-            "x0": chunk_of_tokens(0),
-            "k1": chunk_of_weights(wk, 1),
-            "q0": chunk_of_weights(wq, 0),
-            "q1": chunk_of_weights(wq, 1),
-            "x1": chunk_of_tokens(1),
+            "k0": (chunk_of_weights(wk, 0), TILES),
+            "x0": (chunk_of_tokens(0), TILES),
+            "k1": (chunk_of_weights(wk, 1), 2),
+            "q0": (chunk_of_weights(wq, 0), 2),
+            "q1": (chunk_of_weights(wq, 1), 1),
+            "x1": (chunk_of_tokens(1), 1),
         }
         raw = {}
         in_codes = {}
         in_scales = {}
-        for name, source in sources.items():
+        for name, (source, pieces) in sources.items():
             raw[name] = keep.tile([P, TILES * D], BF16, name="raw_" + name)
             in_codes[name] = keep.tile(
                 [P, TILES * PASSES * P], U32, name="codes_" + name, align_bytes=64
@@ -77,63 +77,64 @@ def tile_attentionnet_pa_kernel(tc, x, wq, wk, out):
                 [P, TILES * PASSES * P], U8, name="scales_" + name, align_bytes=64
             )
             rows = raw[name][:].rearrange("p (r k) -> p r k", r=TILES)
-            if name in ("k0", "x0"):
-                for r in range(TILES):
-                    nc.sync.dma_start(out=rows[:, r, :], in_=source[:, r, :])
-            else:
-                nc.sync.dma_start(out=rows, in_=source)
+            step = TILES // pieces
+            for r in range(0, TILES, step):
+                nc.sync.dma_start(out=rows[:, r : r + step, :], in_=source[:, r : r + step, :])
 
         def block(codes_or_scales, r, c):
             first = (r * PASSES + c) * P
             return codes_or_scales[:, first : first + P]
 
-        def empty_bank(n, dst, src):
-            if n % 4 == 1:
-                nc.vector.tensor_copy(out=dst, in_=src)
-            else:
-                nc.scalar.copy(out=dst, in_=src)
+        sorted_words = {}
+        grouped_in = {}
 
-        def transpose_chunk(name, loads_set_the_pace=False):
-            words = raw[name][:].bitcast(F32)
-            grouped = {}
+        def sort_words(name, r):
+            first = r * WORDS
+            sorted_words[name, r] = stage.tile(
+                [P, PASSES, 2, P], F32, name="sorted_words", tag="sorted_words"
+            )
+            nc.vector.tensor_copy(
+                out=sorted_words[name, r][:],
+                in_=raw[name][:]
+                .bitcast(F32)[:, first : first + WORDS]
+                .rearrange("p (c w u) -> p c u w", c=PASSES, u=2),
+            )
 
-            def quantise(r):
-                first = r * PASSES * P
-                nc.vector.quantize_mx(
-                    out=in_codes[name][:, first : first + PASSES * P].bitcast(FP8X4),
-                    scales=in_scales[name][:, first : first + PASSES * P],
-                    in_=grouped[r][:],
-                )
+        def transpose_rows(name, r):
+            bank = work.tile([P, PASSES, 2, P], F32, tag="work")
+            for c in range(PASSES):
+                for u in range(2):
+                    nc.tensor.transpose(
+                        bank[:, c, u, :], sorted_words[name, r][:, c, u, :], identity[:]
+                    )
+            grouped_in[name, r] = stage.tile(
+                [P, PASSES * P * PACK], BF16, name="grouped_in", tag="grouped_in", align_bytes=64
+            )
+            nc.scalar.copy(
+                out=grouped_in[name, r][:]
+                .bitcast(F32)
+                .rearrange("p (c r u) -> p c r u", c=PASSES, u=2),
+                in_=bank[:].rearrange("p c u r -> p c r u"),
+            )
 
+        def quantise_rows(name, r):
+            first = r * PASSES * P
+            nc.vector.quantize_mx(
+                out=in_codes[name][:, first : first + PASSES * P].bitcast(FP8X4),
+                scales=in_scales[name][:, first : first + PASSES * P],
+                in_=grouped_in[name, r][:],
+            )
+
+        def sort_half(name, half):
+            sort_words(name, 2 * half)
+            sort_words(name, 2 * half + 1)
+
+        def transpose_chunk(name):
             for r in range(TILES):
-                bank = work.tile([P, PASSES, 2, P], F32, tag="work")
-                for c in range(PASSES):
-                    for u in range(2):
-                        first = r * WORDS + 2 * c * P
-                        nc.tensor.transpose(
-                            bank[:, c, u, :],
-                            words[:, first + u : first + 2 * P : 2],
-                            identity[:],
-                        )
-                if loads_set_the_pace:
-                    keep_tensor_engine_busy(1)
-                grouped[r] = stage.tile(
-                    [P, PASSES * P * PACK],
-                    BF16,
-                    name="grouped_in",
-                    tag="grouped_in",
-                    align_bytes=64,
-                )
-                empty_bank(
-                    r,
-                    grouped[r][:]
-                    .bitcast(F32)
-                    .rearrange("p (c r u) -> p c r u", c=PASSES, u=2),
-                    bank[:].rearrange("p c u r -> p c r u"),
-                )
+                transpose_rows(name, r)
                 if r > 0:
-                    quantise(r - 1)
-            quantise(TILES - 1)
+                    quantise_rows(name, r - 1)
+            quantise_rows(name, TILES - 1)
 
         qk_codes = {}
         qk_scales = {}
@@ -146,11 +147,11 @@ def tile_attentionnet_pa_kernel(tc, x, wq, wk, out):
                     [P, PASSES * S], U8, name="proj_scales_%s%d" % (name, b), align_bytes=64
                 )
 
-        def project_pair(name, b, pair, n):
-            xb = "x%d" % b
+        def project(banks, on_vector):
             grouped = {}
-            for m, (g, i) in enumerate(pair):
+            for m, (name, g, b, i) in enumerate(banks):
                 w = "%s%d" % (name, g)
+                xb = "x%d" % b
                 bank = work.tile([P, PACK, P], F32, tag="work")
                 for t in range(PACK):
                     for c in range(PASSES):
@@ -166,25 +167,19 @@ def tile_attentionnet_pa_kernel(tc, x, wq, wk, out):
                 grouped[m] = stage.tile(
                     [P, P * PACK], BF16, name="grouped_qk", tag="grouped_qk", align_bytes=64
                 )
-                empty_bank(
-                    n + m,
-                    grouped[m][:].rearrange("p (r t) -> p r t", t=PACK),
-                    bank[:].rearrange("p t r -> p r t"),
-                )
-            for m, (g, i) in enumerate(pair):
+                dst = grouped[m][:].rearrange("p (r t) -> p r t", t=PACK)
+                src = bank[:].rearrange("p t r -> p r t")
+                if m == on_vector:
+                    nc.vector.tensor_copy(out=dst, in_=src)
+                else:
+                    nc.scalar.copy(out=dst, in_=src)
+            for m, (name, g, b, i) in enumerate(banks):
                 first = g * S + i * P
                 nc.vector.quantize_mx(
                     out=qk_codes[name, b][:, first : first + P].bitcast(FP8X4),
                     scales=qk_scales[name, b][:, first : first + P],
                     in_=grouped[m][:],
                 )
-
-        def project_keys(g, b):
-            project_pair("k", b, [(g, 0), (g, 1)], 0)
-            project_pair("k", b, [(g, 2), (g, 3)], 2)
-
-        def project_queries(b, i):
-            project_pair("q", b, [(0, i), (1, i)], 2 * (i % 2))
 
         score = {}
         shift = {}
@@ -234,24 +229,53 @@ def tile_attentionnet_pa_kernel(tc, x, wq, wk, out):
             nc.sync.dma_start(out=out[b, i * P : (i + 1) * P, :], in_=weights[b, i][:])
 
         keep_tensor_engine_busy(WARM_UP)
-        transpose_chunk("k0", loads_set_the_pace=True)
-        transpose_chunk("x0", loads_set_the_pace=True)
-        project_keys(0, 0)
-        transpose_chunk("k1")
-        transpose_chunk("q0")
-        project_keys(1, 0)
-        transpose_chunk("q1")
-        transpose_chunk("x1")
-        tiles = [(b, i) for b in range(B) for i in range(TILES)]
-        for n in range(len(tiles) + 2):
-            if n < len(tiles):
-                b, i = tiles[n]
-                if b > 0 and i == 0:
-                    project_keys(0, b)
-                    project_keys(1, b)
-                project_queries(b, i)
-            if 1 <= n <= len(tiles):
-                scores_and_max(*tiles[n - 1])
+        first_rows = [(name, r) for name in ("k0", "x0") for r in range(TILES)]
+        for n, (name, r) in enumerate(first_rows):
+            sort_words(name, r)
+            transpose_rows(name, r)
+            keep_tensor_engine_busy(1)
             if n >= 2:
-                exponentials(*tiles[n - 2])
-                normalise_and_store(*tiles[n - 2])
+                quantise_rows(*first_rows[n - 2])
+        quantise_rows(*first_rows[-2])
+        quantise_rows(*first_rows[-1])
+
+        def project_half(name, g, half):
+            project([(name, g, 0, 2 * half), (name, g, 0, 2 * half + 1)], 1 - 2 * half)
+
+        sort_half("k1", 0)
+        project_half("k", 0, 0)
+        sort_half("k1", 1)
+        transpose_chunk("k1")
+        sort_half("q0", 0)
+        project_half("k", 0, 1)
+        sort_half("q0", 1)
+        transpose_chunk("q0")
+        sort_half("q1", 0)
+        project_half("k", 1, 0)
+        sort_half("q1", 1)
+        project_half("k", 1, 1)
+        transpose_chunk("q1")
+        sort_half("x1", 0)
+        project_half("q", 0, 0)
+        sort_half("x1", 1)
+        project_half("q", 0, 1)
+        transpose_chunk("x1")
+
+        steps = [([("q", 1, 0, i), ("k", 0, 1, i)], [(0, i - 1)] if i else []) for i in range(TILES)]
+        steps += [([("k", 1, 1, 0), ("k", 1, 1, 1)], [(0, 3)])]
+        steps += [([("k", 1, 1, 2), ("k", 1, 1, 3)], [])]
+        steps += [([("q", 0, 1, i), ("q", 1, 1, i)], []) for i in range(2)]
+        steps += [([("q", 0, 1, 2), ("q", 1, 1, 2)], [(1, 0)])]
+        steps += [([("q", 0, 1, 3), ("q", 1, 1, 3)], [(1, 1), (1, 2), (1, 3)])]
+        waiting = []
+        for banks, tiles in steps:
+            project(banks, None if tiles else 1)
+            for tile in tiles:
+                scores_and_max(*tile)
+                waiting.append(tile)
+                if len(waiting) > 1:
+                    exponentials(*waiting[0])
+                    normalise_and_store(*waiting[0])
+                    waiting = waiting[1:]
+        exponentials(*waiting[0])
+        normalise_and_store(*waiting[0])

@@ -19,7 +19,7 @@ PASSES = D // K_PASS
 TILES = S // P
 WORDS = D // 2
 INV_SQRT = 1.0 / math.sqrt(D // 8)
-WARM_UP = 6
+WARM_UP = 4
 
 FLOPS = 2 * (2 * B * S * D * D) + 2 * B * S * S * D
 
@@ -28,7 +28,7 @@ def tile_attentionnet_pa_kernel(tc, x, wq, wk, out):
     nc = tc.nc
     with ExitStack() as ctx:
         keep = ctx.enter_context(tc.tile_pool(name="keep", bufs=1))
-        stage = ctx.enter_context(tc.tile_pool(name="stage", bufs=6))
+        stage = ctx.enter_context(tc.tile_pool(name="stage", bufs=8))
         small = ctx.enter_context(tc.tile_pool(name="small", bufs=4))
         work = ctx.enter_context(tc.psum_pool(name="work", bufs=5))
         score_pool = ctx.enter_context(tc.psum_pool(name="score_pool", bufs=3))
@@ -44,12 +44,15 @@ def tile_attentionnet_pa_kernel(tc, x, wq, wk, out):
         zeros = keep.tile([P, S], BF16, name="zeros")
         nc.vector.memset(zeros[:], 0.0)
 
-        def keep_tensor_engine_busy(count):
-            for n in range(count):
-                unread = work.tile([P, S], F32, tag="work")
-                nc.tensor.matmul(
-                    out=unread[:], lhsT=zeros[:, :P], rhs=zeros[:], start=True, stop=True
-                )
+        def keep_tensor_engine_busy(width):
+            unread = work.tile([P, S], F32, tag="work")
+            nc.tensor.matmul(
+                out=unread[:, :width],
+                lhsT=zeros[:, :P],
+                rhs=zeros[:, :width],
+                start=True,
+                stop=True,
+            )
 
         def chunk_of_weights(w, g):
             return w.rearrange("(g p j) k -> g p j k", p=P, j=PACK)[g]
@@ -102,11 +105,15 @@ def tile_attentionnet_pa_kernel(tc, x, wq, wk, out):
 
         def transpose_rows(name, r):
             bank = work.tile([P, PASSES, 2, P], F32, tag="work")
+            words = raw[name][:].bitcast(F32)
             for c in range(PASSES):
                 for u in range(2):
-                    nc.tensor.transpose(
-                        bank[:, c, u, :], sorted_words[name, r][:, c, u, :], identity[:]
-                    )
+                    first = r * WORDS + 2 * c * P
+                    if (name, r) in sorted_words:
+                        columns = sorted_words[name, r][:, c, u, :]
+                    else:
+                        columns = words[:, first + u : first + 2 * P : 2]
+                    nc.tensor.transpose(bank[:, c, u, :], columns, identity[:])
             grouped_in[name, r] = stage.tile(
                 [P, PASSES * P * PACK], BF16, name="grouped_in", tag="grouped_in", align_bytes=64
             )
@@ -125,9 +132,11 @@ def tile_attentionnet_pa_kernel(tc, x, wq, wk, out):
                 in_=grouped_in[name, r][:],
             )
 
-        def sort_half(name, half):
-            sort_words(name, 2 * half)
-            sort_words(name, 2 * half + 1)
+        to_sort = [(name, r) for name in ("k1", "q0", "q1", "x1") for r in range(TILES)]
+
+        def sort_ahead(count):
+            for n in range(min(count, len(to_sort))):
+                sort_words(*to_sort.pop(0))
 
         def transpose_chunk(name):
             for r in range(TILES):
@@ -182,9 +191,11 @@ def tile_attentionnet_pa_kernel(tc, x, wq, wk, out):
                 )
 
         score = {}
+        row_max = {}
         shift = {}
         weights = {}
         row_sum = {}
+        inverse = {}
 
         def scores_and_max(b, i):
             score[b, i] = score_pool.tile([P, S], F32, name="score", tag="score")
@@ -199,13 +210,15 @@ def tile_attentionnet_pa_kernel(tc, x, wq, wk, out):
                     start=(g == 0),
                     stop=(g == PASSES - 1),
                 )
-            row_max = small.tile([P, 1], F32, tag="row_max")
+            row_max[b, i] = small.tile([P, 1], F32, name="row_max", tag="row_max")
             nc.vector.reduce_max(
-                out=row_max[:], in_=score[b, i][:], axis=mybir.AxisListType.X
+                out=row_max[b, i][:], in_=score[b, i][:], axis=mybir.AxisListType.X
             )
+
+        def shift_of_max(b, i):
             shift[b, i] = small.tile([P, 1], F32, name="shift", tag="shift")
             nc.vector.tensor_scalar_mul(
-                out=shift[b, i][:], in0=row_max[:], scalar1=-INV_SQRT
+                out=shift[b, i][:], in0=row_max[b, i][:], scalar1=-INV_SQRT
             )
 
         def exponentials(b, i):
@@ -220,62 +233,82 @@ def tile_attentionnet_pa_kernel(tc, x, wq, wk, out):
                 accum_out=row_sum[b, i][:],
             )
 
+        def invert_sum(b, i):
+            inverse[b, i] = small.tile([P, 1], F32, name="inverse", tag="inverse")
+            nc.vector.reciprocal(out=inverse[b, i][:], in_=row_sum[b, i][:])
+
         def normalise_and_store(b, i):
-            inverse = small.tile([P, 1], F32, tag="inverse")
-            nc.vector.reciprocal(out=inverse[:], in_=row_sum[b, i][:])
             nc.vector.tensor_scalar_mul(
-                out=weights[b, i][:], in0=weights[b, i][:], scalar1=inverse[:]
+                out=weights[b, i][:], in0=weights[b, i][:], scalar1=inverse[b, i][:]
             )
             nc.sync.dma_start(out=out[b, i * P : (i + 1) * P, :], in_=weights[b, i][:])
 
-        keep_tensor_engine_busy(WARM_UP)
+        for n in range(WARM_UP):
+            keep_tensor_engine_busy(S)
         first_rows = [(name, r) for name in ("k0", "x0") for r in range(TILES)]
+        sort_words(*first_rows[1])
         for n, (name, r) in enumerate(first_rows):
-            sort_words(name, r)
             transpose_rows(name, r)
-            keep_tensor_engine_busy(1)
-            if n >= 2:
-                quantise_rows(*first_rows[n - 2])
-        quantise_rows(*first_rows[-2])
+            keep_tensor_engine_busy(256)
+            if n >= 1:
+                quantise_rows(*first_rows[n - 1])
+            if n + 2 < len(first_rows):
+                sort_words(*first_rows[n + 2])
+            else:
+                sort_ahead(1)
         quantise_rows(*first_rows[-1])
 
         def project_half(name, g, half):
             project([(name, g, 0, 2 * half), (name, g, 0, 2 * half + 1)], 1 - 2 * half)
 
-        sort_half("k1", 0)
+        sort_ahead(2)
         project_half("k", 0, 0)
-        sort_half("k1", 1)
+        sort_ahead(2)
         transpose_chunk("k1")
-        sort_half("q0", 0)
+        sort_ahead(2)
         project_half("k", 0, 1)
-        sort_half("q0", 1)
+        sort_ahead(2)
         transpose_chunk("q0")
-        sort_half("q1", 0)
+        sort_ahead(2)
         project_half("k", 1, 0)
-        sort_half("q1", 1)
+        sort_ahead(2)
         project_half("k", 1, 1)
         transpose_chunk("q1")
-        sort_half("x1", 0)
+        sort_ahead(2)
         project_half("q", 0, 0)
-        sort_half("x1", 1)
+        sort_ahead(2)
         project_half("q", 0, 1)
+        sort_ahead(4)
         transpose_chunk("x1")
 
-        steps = [([("q", 1, 0, i), ("k", 0, 1, i)], [(0, i - 1)] if i else []) for i in range(TILES)]
-        steps += [([("k", 1, 1, 0), ("k", 1, 1, 1)], [(0, 3)])]
-        steps += [([("k", 1, 1, 2), ("k", 1, 1, 3)], [])]
-        steps += [([("q", 0, 1, i), ("q", 1, 1, i)], []) for i in range(2)]
-        steps += [([("q", 0, 1, 2), ("q", 1, 1, 2)], [(1, 0)])]
-        steps += [([("q", 0, 1, 3), ("q", 1, 1, 3)], [(1, 1), (1, 2), (1, 3)])]
-        waiting = []
-        for banks, tiles in steps:
-            project(banks, None if tiles else 1)
-            for tile in tiles:
-                scores_and_max(*tile)
-                waiting.append(tile)
-                if len(waiting) > 1:
-                    exponentials(*waiting[0])
-                    normalise_and_store(*waiting[0])
-                    waiting = waiting[1:]
-        exponentials(*waiting[0])
-        normalise_and_store(*waiting[0])
+        tiles = [(b, i) for b in range(B) for i in range(TILES)]
+
+        def softmax_step(n):
+            if n < len(tiles):
+                scores_and_max(*tiles[n])
+            if n >= 2:
+                invert_sum(*tiles[n - 2])
+            if n < len(tiles):
+                shift_of_max(*tiles[n])
+            if n >= 2:
+                normalise_and_store(*tiles[n - 2])
+            if 1 <= n <= len(tiles):
+                exponentials(*tiles[n - 1])
+
+        for i in range(TILES):
+            project([("q", 1, 0, i), ("k", 0, 1, i)], None if i else 1)
+            if i:
+                softmax_step(i - 1)
+        project([("k", 1, 1, 0), ("k", 1, 1, 1)], None)
+        softmax_step(3)
+        project([("k", 1, 1, 2), ("k", 1, 1, 3)], 1)
+        project([("q", 0, 1, 0), ("q", 1, 1, 0)], 1)
+        project([("q", 0, 1, 1), ("q", 1, 1, 1)], None)
+        softmax_step(4)
+        project([("q", 0, 1, 2), ("q", 1, 1, 2)], None)
+        softmax_step(5)
+        project([("q", 0, 1, 3), ("q", 1, 1, 3)], None)
+        softmax_step(6)
+        softmax_step(7)
+        softmax_step(8)
+        softmax_step(9)

@@ -10,6 +10,7 @@ U32 = mybir.dt.uint32
 U8 = mybir.dt.uint8
 FP8X4 = mybir.dt.float8_e4m3fn_x4
 EXP = mybir.ActivationFunctionType.Exp
+ALU = mybir.AluOpType
 
 P = 128
 PACK = 4
@@ -19,7 +20,7 @@ PASSES = D // K_PASS
 TILES = S // P
 WORDS = D // 2
 INV_SQRT = 1.0 / math.sqrt(D // 8)
-WARM_UP = 4
+UNSORTED = 8
 
 FLOPS = 2 * (2 * B * S * D * D) + 2 * B * S * S * D
 
@@ -41,37 +42,29 @@ def tile_attentionnet_pa_kernel(tc, x, wq, wk, out):
         nc.vector.memset(zero[:], 0.0)
         nc.scalar.activation(out=one[:], in_=zero[:], func=EXP)
 
-        zeros = keep.tile([P, S], BF16, name="zeros")
-        nc.vector.memset(zeros[:], 0.0)
-
-        def keep_tensor_engine_busy(width):
-            unread = work.tile([P, S], F32, tag="work")
-            nc.tensor.matmul(
-                out=unread[:, :width],
-                lhsT=zeros[:, :P],
-                rhs=zeros[:, :width],
-                start=True,
-                stop=True,
-            )
-
         def chunk_of_weights(w, g):
             return w.rearrange("(g p j) k -> g p j k", p=P, j=PACK)[g]
 
         def chunk_of_tokens(b):
             return x[b].rearrange("(i p) k -> p i k", p=P)
 
+        loads = [("x0", 0, 1), ("x0", 1, 1)]
+        loads += [("k0", r, 1) for r in range(TILES)]
+        loads += [("x0", 2, 1), ("x0", 3, 1)]
+        loads += [(name, r, 2) for name in ("k1", "q0") for r in (0, 2)]
+        loads += [("q1", 0, TILES), ("x1", 0, TILES)]
         sources = {
-            "k0": (chunk_of_weights(wk, 0), TILES),
-            "x0": (chunk_of_tokens(0), TILES),
-            "k1": (chunk_of_weights(wk, 1), 2),
-            "q0": (chunk_of_weights(wq, 0), 2),
-            "q1": (chunk_of_weights(wq, 1), 1),
-            "x1": (chunk_of_tokens(1), 1),
+            "x0": chunk_of_tokens(0),
+            "k0": chunk_of_weights(wk, 0),
+            "k1": chunk_of_weights(wk, 1),
+            "q0": chunk_of_weights(wq, 0),
+            "q1": chunk_of_weights(wq, 1),
+            "x1": chunk_of_tokens(1),
         }
         raw = {}
         in_codes = {}
         in_scales = {}
-        for name, (source, pieces) in sources.items():
+        for name in sources:
             raw[name] = keep.tile([P, TILES * D], BF16, name="raw_" + name)
             in_codes[name] = keep.tile(
                 [P, TILES * PASSES * P], U32, name="codes_" + name, align_bytes=64
@@ -79,10 +72,11 @@ def tile_attentionnet_pa_kernel(tc, x, wq, wk, out):
             in_scales[name] = keep.tile(
                 [P, TILES * PASSES * P], U8, name="scales_" + name, align_bytes=64
             )
+        for name, r, count in loads:
             rows = raw[name][:].rearrange("p (r k) -> p r k", r=TILES)
-            step = TILES // pieces
-            for r in range(0, TILES, step):
-                nc.sync.dma_start(out=rows[:, r : r + step, :], in_=source[:, r : r + step, :])
+            nc.sync.dma_start(
+                out=rows[:, r : r + count, :], in_=sources[name][:, r : r + count, :]
+            )
 
         def block(codes_or_scales, r, c):
             first = (r * PASSES + c) * P
@@ -132,7 +126,8 @@ def tile_attentionnet_pa_kernel(tc, x, wq, wk, out):
                 in_=grouped_in[name, r][:],
             )
 
-        to_sort = [(name, r) for name in ("k1", "q0", "q1", "x1") for r in range(TILES)]
+        row_order = [(name, r) for name, first, count in loads for r in range(first, first + count)]
+        to_sort = row_order[UNSORTED:]
 
         def sort_ahead(count):
             for n in range(min(count, len(to_sort))):
@@ -156,48 +151,61 @@ def tile_attentionnet_pa_kernel(tc, x, wq, wk, out):
                     [P, PASSES * S], U8, name="proj_scales_%s%d" % (name, b), align_bytes=64
                 )
 
-        def project(banks, on_vector):
-            grouped = {}
-            for m, (name, g, b, i) in enumerate(banks):
-                w = "%s%d" % (name, g)
-                xb = "x%d" % b
-                bank = work.tile([P, PACK, P], F32, tag="work")
-                for t in range(PACK):
-                    for c in range(PASSES):
-                        nc.tensor.matmul_mx(
-                            out=bank[:, t, :],
-                            lhsT=block(in_codes[w], t, c).bitcast(FP8X4),
-                            lhsT_scale=block(in_scales[w], t, c),
-                            rhs=block(in_codes[xb], i, c).bitcast(FP8X4),
-                            rhs_scale=block(in_scales[xb], i, c),
-                            start=(c == 0),
-                            stop=(c == PASSES - 1),
-                        )
-                grouped[m] = stage.tile(
+        open_banks = {}
+
+        def multiply(name, g, b, i, features):
+            w = "%s%d" % (name, g)
+            xb = "x%d" % b
+            if features[0] == 0:
+                open_banks[name, g, b, i] = work.tile([P, PACK, P], F32, name="bank", tag="work")
+            for t in features:
+                for c in range(PASSES):
+                    nc.tensor.matmul_mx(
+                        out=open_banks[name, g, b, i][:, t, :],
+                        lhsT=block(in_codes[w], t, c).bitcast(FP8X4),
+                        lhsT_scale=block(in_scales[w], t, c),
+                        rhs=block(in_codes[xb], i, c).bitcast(FP8X4),
+                        rhs_scale=block(in_scales[xb], i, c),
+                        start=(c == 0),
+                        stop=(c == PASSES - 1),
+                    )
+
+        grouped_qk = {}
+
+        def empty_projected(banks, on_vector):
+            for n, bank in enumerate(banks):
+                grouped_qk[bank] = stage.tile(
                     [P, P * PACK], BF16, name="grouped_qk", tag="grouped_qk", align_bytes=64
                 )
-                dst = grouped[m][:].rearrange("p (r t) -> p r t", t=PACK)
-                src = bank[:].rearrange("p t r -> p r t")
-                if m == on_vector:
+                dst = grouped_qk[bank][:].rearrange("p (r t) -> p r t", t=PACK)
+                src = open_banks[bank][:].rearrange("p t r -> p r t")
+                if n in on_vector:
                     nc.vector.tensor_copy(out=dst, in_=src)
                 else:
                     nc.scalar.copy(out=dst, in_=src)
-            for m, (name, g, b, i) in enumerate(banks):
+
+        def quantise_projected(banks):
+            for name, g, b, i in banks:
                 first = g * S + i * P
                 nc.vector.quantize_mx(
                     out=qk_codes[name, b][:, first : first + P].bitcast(FP8X4),
                     scales=qk_scales[name, b][:, first : first + P],
-                    in_=grouped[m][:],
+                    in_=grouped_qk[name, g, b, i][:],
                 )
 
+        def project(banks, on_vector):
+            for bank in banks:
+                multiply(*bank, range(PACK))
+            empty_projected(banks, on_vector)
+            quantise_projected(banks)
+
         score = {}
-        row_max = {}
         shift = {}
         weights = {}
         row_sum = {}
         inverse = {}
 
-        def scores_and_max(b, i):
+        def scores_and_shift(b, i):
             score[b, i] = score_pool.tile([P, S], F32, name="score", tag="score")
             for g in range(PASSES):
                 first = g * S + i * P
@@ -210,15 +218,16 @@ def tile_attentionnet_pa_kernel(tc, x, wq, wk, out):
                     start=(g == 0),
                     stop=(g == PASSES - 1),
                 )
-            row_max[b, i] = small.tile([P, 1], F32, name="row_max", tag="row_max")
-            nc.vector.reduce_max(
-                out=row_max[b, i][:], in_=score[b, i][:], axis=mybir.AxisListType.X
-            )
-
-        def shift_of_max(b, i):
             shift[b, i] = small.tile([P, 1], F32, name="shift", tag="shift")
-            nc.vector.tensor_scalar_mul(
-                out=shift[b, i][:], in0=row_max[b, i][:], scalar1=-INV_SQRT
+            unread = stage.tile([P, S], F32, name="unread_products", tag="unread_products")
+            nc.vector.tensor_scalar(
+                out=unread[:],
+                in0=score[b, i][:],
+                scalar1=-INV_SQRT,
+                scalar2=None,
+                op0=ALU.mult,
+                op1=ALU.min,
+                accum_out=shift[b, i][:],
             )
 
         def exponentials(b, i):
@@ -237,78 +246,143 @@ def tile_attentionnet_pa_kernel(tc, x, wq, wk, out):
             inverse[b, i] = small.tile([P, 1], F32, name="inverse", tag="inverse")
             nc.vector.reciprocal(out=inverse[b, i][:], in_=row_sum[b, i][:])
 
-        def normalise_and_store(b, i):
-            nc.vector.tensor_scalar_mul(
-                out=weights[b, i][:], in0=weights[b, i][:], scalar1=inverse[b, i][:]
+        def normalise_and_store(b, i, engine):
+            engine.tensor_scalar(
+                out=weights[b, i][:],
+                in0=weights[b, i][:],
+                scalar1=inverse[b, i][:],
+                scalar2=0.0,
+                op0=ALU.mult,
+                op1=ALU.add,
             )
             nc.sync.dma_start(out=out[b, i * P : (i + 1) * P, :], in_=weights[b, i][:])
 
-        for n in range(WARM_UP):
-            keep_tensor_engine_busy(S)
-        first_rows = [(name, r) for name in ("k0", "x0") for r in range(TILES)]
-        sort_words(*first_rows[1])
-        for n, (name, r) in enumerate(first_rows):
-            transpose_rows(name, r)
-            keep_tensor_engine_busy(256)
-            if n >= 1:
-                quantise_rows(*first_rows[n - 1])
-            if n + 2 < len(first_rows):
-                sort_words(*first_rows[n + 2])
-            else:
-                sort_ahead(1)
-        quantise_rows(*first_rows[-1])
+        def transpose_pair(n):
+            for name, r in row_order[n : n + 2]:
+                transpose_rows(name, r)
 
-        def project_half(name, g, half):
-            project([(name, g, 0, 2 * half), (name, g, 0, 2 * half + 1)], 1 - 2 * half)
-
-        sort_ahead(2)
-        project_half("k", 0, 0)
-        sort_ahead(2)
-        transpose_chunk("k1")
-        sort_ahead(2)
-        project_half("k", 0, 1)
-        sort_ahead(2)
-        transpose_chunk("q0")
-        sort_ahead(2)
-        project_half("k", 1, 0)
-        sort_ahead(2)
-        project_half("k", 1, 1)
-        transpose_chunk("q1")
-        sort_ahead(2)
-        project_half("q", 0, 0)
-        sort_ahead(2)
-        project_half("q", 0, 1)
-        sort_ahead(4)
-        transpose_chunk("x1")
+        def quantise_pair(n):
+            for name, r in row_order[n : n + 2]:
+                quantise_rows(name, r)
 
         tiles = [(b, i) for b in range(B) for i in range(TILES)]
 
-        def softmax_step(n):
-            if n < len(tiles):
-                scores_and_max(*tiles[n])
-            if n >= 2:
-                invert_sum(*tiles[n - 2])
-            if n < len(tiles):
-                shift_of_max(*tiles[n])
-            if n >= 2:
-                normalise_and_store(*tiles[n - 2])
-            if 1 <= n <= len(tiles):
-                exponentials(*tiles[n - 1])
-
-        for i in range(TILES):
-            project([("q", 1, 0, i), ("k", 0, 1, i)], None if i else 1)
-            if i:
-                softmax_step(i - 1)
-        project([("k", 1, 1, 0), ("k", 1, 1, 1)], None)
-        softmax_step(3)
-        project([("k", 1, 1, 2), ("k", 1, 1, 3)], 1)
-        project([("q", 0, 1, 0), ("q", 1, 1, 0)], 1)
-        project([("q", 0, 1, 1), ("q", 1, 1, 1)], None)
-        softmax_step(4)
-        project([("q", 0, 1, 2), ("q", 1, 1, 2)], None)
-        softmax_step(5)
-        project([("q", 0, 1, 3), ("q", 1, 1, 3)], None)
-        softmax_step(6)
-        softmax_step(7)
-        softmax_step(8)
-        softmax_step(9)
+        transpose_rows(*row_order[0])
+        transpose_rows(*row_order[1])
+        quantise_rows(*row_order[0])
+        transpose_rows(*row_order[2])
+        quantise_rows(*row_order[1])
+        transpose_rows(*row_order[3])
+        quantise_rows(*row_order[2])
+        transpose_rows(*row_order[4])
+        quantise_rows(*row_order[3])
+        transpose_rows(*row_order[5])
+        quantise_rows(*row_order[4])
+        sort_ahead(1)
+        transpose_pair(6)
+        quantise_rows(*row_order[5])
+        sort_ahead(1)
+        multiply(*("k", 0, 0, 0), [0])
+        multiply(*("k", 0, 0, 1), [0])
+        multiply(*("k", 0, 0, 0), [1])
+        multiply(*("k", 0, 0, 1), [1])
+        quantise_pair(6)
+        sort_ahead(2)
+        multiply(*("k", 0, 0, 0), [2,3])
+        multiply(*("k", 0, 0, 1), [2,3])
+        empty_projected([("k", 0, 0, 0), ("k", 0, 0, 1)], [])
+        transpose_pair(8)
+        quantise_projected([("k", 0, 0, 0), ("k", 0, 0, 1)])
+        sort_ahead(2)
+        quantise_pair(8)
+        multiply(*("k", 0, 0, 2), range(PACK))
+        multiply(*("k", 0, 0, 3), range(PACK))
+        empty_projected([("k", 0, 0, 2), ("k", 0, 0, 3)], [0])
+        transpose_pair(10)
+        sort_ahead(2)
+        quantise_projected([("k", 0, 0, 2), ("k", 0, 0, 3)])
+        quantise_pair(10)
+        sort_ahead(2)
+        transpose_pair(12)
+        transpose_pair(14)
+        multiply(*("k", 1, 0, 0), range(PACK))
+        multiply(*("k", 1, 0, 1), range(PACK))
+        empty_projected([("k", 1, 0, 0), ("k", 1, 0, 1)], [1])
+        quantise_pair(12)
+        sort_ahead(2)
+        quantise_pair(14)
+        quantise_projected([("k", 1, 0, 0), ("k", 1, 0, 1)])
+        sort_ahead(2)
+        project([("k", 1, 0, 2), ("k", 1, 0, 3)], [])
+        transpose_pair(16)
+        transpose_pair(18)
+        sort_ahead(2)
+        quantise_pair(16)
+        multiply(*("q", 0, 0, 0), range(PACK))
+        multiply(*("q", 0, 0, 1), range(PACK))
+        empty_projected([("q", 0, 0, 0), ("q", 0, 0, 1)], [1])
+        quantise_pair(18)
+        quantise_projected([("q", 0, 0, 0), ("q", 0, 0, 1)])
+        sort_ahead(2)
+        project([("q", 0, 0, 2), ("q", 0, 0, 3)], [])
+        transpose_pair(20)
+        transpose_pair(22)
+        quantise_pair(20)
+        multiply(*("q", 1, 0, 0), range(PACK))
+        multiply(*("k", 0, 1, 0), range(PACK))
+        empty_projected([("q", 1, 0, 0), ("k", 0, 1, 0)], [1])
+        quantise_pair(22)
+        quantise_projected([("q", 1, 0, 0), ("k", 0, 1, 0)])
+        project([("q", 1, 0, 1), ("k", 0, 1, 1)], [])
+        scores_and_shift(*tiles[0])
+        project([("q", 1, 0, 2), ("k", 0, 1, 2)], [])
+        scores_and_shift(*tiles[1])
+        exponentials(*tiles[0])
+        project([("q", 1, 0, 3), ("k", 0, 1, 3)], [])
+        scores_and_shift(*tiles[2])
+        invert_sum(*tiles[0])
+        exponentials(*tiles[1])
+        multiply(*("k", 1, 1, 0), range(PACK))
+        multiply(*("k", 1, 1, 1), range(PACK))
+        empty_projected([("k", 1, 1, 0), ("k", 1, 1, 1)], [])
+        normalise_and_store(*tiles[0], nc.vector)
+        quantise_projected([("k", 1, 1, 0), ("k", 1, 1, 1)])
+        scores_and_shift(*tiles[3])
+        invert_sum(*tiles[1])
+        exponentials(*tiles[2])
+        multiply(*("k", 1, 1, 2), range(PACK))
+        multiply(*("k", 1, 1, 3), range(PACK))
+        empty_projected([("k", 1, 1, 2), ("k", 1, 1, 3)], [1])
+        normalise_and_store(*tiles[1], nc.vector)
+        quantise_projected([("k", 1, 1, 2), ("k", 1, 1, 3)])
+        invert_sum(*tiles[2])
+        exponentials(*tiles[3])
+        multiply(*("q", 0, 1, 0), range(PACK))
+        multiply(*("q", 1, 1, 0), range(PACK))
+        empty_projected([("q", 0, 1, 0), ("q", 1, 1, 0)], [1])
+        normalise_and_store(*tiles[2], nc.vector)
+        quantise_projected([("q", 0, 1, 0), ("q", 1, 1, 0)])
+        invert_sum(*tiles[3])
+        multiply(*("q", 0, 1, 1), range(PACK))
+        multiply(*("q", 1, 1, 1), range(PACK))
+        empty_projected([("q", 0, 1, 1), ("q", 1, 1, 1)], [1])
+        normalise_and_store(*tiles[3], nc.vector)
+        quantise_projected([("q", 0, 1, 1), ("q", 1, 1, 1)])
+        project([("q", 0, 1, 2), ("q", 1, 1, 2)], [1])
+        scores_and_shift(*tiles[4])
+        project([("q", 0, 1, 3), ("q", 1, 1, 3)], [1])
+        scores_and_shift(*tiles[5])
+        exponentials(*tiles[4])
+        scores_and_shift(*tiles[6])
+        invert_sum(*tiles[4])
+        exponentials(*tiles[5])
+        scores_and_shift(*tiles[7])
+        normalise_and_store(*tiles[4], nc.vector)
+        invert_sum(*tiles[5])
+        exponentials(*tiles[6])
+        normalise_and_store(*tiles[5], nc.vector)
+        invert_sum(*tiles[6])
+        exponentials(*tiles[7])
+        normalise_and_store(*tiles[6], nc.vector)
+        invert_sum(*tiles[7])
+        normalise_and_store(*tiles[7], nc.vector)

@@ -20,7 +20,7 @@ PASSES = D // K_PASS
 TILES = S // P
 WORDS = D // 2
 INV_SQRT = 1.0 / math.sqrt(D // 8)
-UNSORTED = 8
+UNSORTED = 24
 
 FLOPS = 2 * (2 * B * S * D * D) + 2 * B * S * S * D
 

@@ -20,7 +20,7 @@ PASSES = D // K_PASS
 TILES = S // P
 WORDS = D // 2
 INV_SQRT = 1.0 / math.sqrt(D // 8)
-UNSORTED = 24
+SQUARE = 32
 
 FLOPS = 2 * (2 * B * S * D * D) + 2 * B * S * S * D
 
@@ -72,7 +72,21 @@ def tile_attentionnet_pa_kernel(tc, x, wq, wk, out):
             in_scales[name] = keep.tile(
                 [P, TILES * PASSES * P], U8, name="scales_" + name, align_bytes=64
             )
+        def load_for_vector():
+            slots = raw["x1"][:].rearrange("p (g c k) -> p g c k", c=PASSES, k=P)
+            tokens = x[1].rearrange("(g j) k -> j g k", j=SQUARE)
+            for c in range(PASSES):
+                for a in range(P // SQUARE):
+                    first = c * K_PASS + a * P
+                    nc.sync.dma_start(
+                        out=slots[SQUARE * a : SQUARE * (a + 1), :, c, :],
+                        in_=tokens[:, :, first : first + P],
+                    )
+
         for name, r, count in loads:
+            if name == "x1":
+                load_for_vector()
+                continue
             rows = raw[name][:].rearrange("p (r k) -> p r k", r=TILES)
             nc.sync.dma_start(
                 out=rows[:, r : r + count, :], in_=sources[name][:, r : r + count, :]
@@ -82,41 +96,71 @@ def tile_attentionnet_pa_kernel(tc, x, wq, wk, out):
             first = (r * PASSES + c) * P
             return codes_or_scales[:, first : first + P]
 
-        sorted_words = {}
         grouped_in = {}
 
-        def sort_words(name, r):
-            first = r * WORDS
-            sorted_words[name, r] = stage.tile(
-                [P, PASSES, 2, P], F32, name="sorted_words", tag="sorted_words"
-            )
-            nc.vector.tensor_copy(
-                out=sorted_words[name, r][:],
-                in_=raw[name][:]
-                .bitcast(F32)[:, first : first + WORDS]
-                .rearrange("p (c w u) -> p c u w", c=PASSES, u=2),
-            )
-
-        def transpose_rows(name, r):
+        def transpose_rows(name, r, on_vector=False):
             bank = work.tile([P, PASSES, 2, P], F32, tag="work")
             words = raw[name][:].bitcast(F32)
             for c in range(PASSES):
                 for u in range(2):
                     first = r * WORDS + 2 * c * P
-                    if (name, r) in sorted_words:
-                        columns = sorted_words[name, r][:, c, u, :]
-                    else:
-                        columns = words[:, first + u : first + 2 * P : 2]
+                    columns = words[:, first + u : first + 2 * P : 2]
                     nc.tensor.transpose(bank[:, c, u, :], columns, identity[:])
             grouped_in[name, r] = stage.tile(
                 [P, PASSES * P * PACK], BF16, name="grouped_in", tag="grouped_in", align_bytes=64
             )
-            nc.scalar.copy(
-                out=grouped_in[name, r][:]
+            dst = (
+                grouped_in[name, r][:]
                 .bitcast(F32)
-                .rearrange("p (c r u) -> p c r u", c=PASSES, u=2),
-                in_=bank[:].rearrange("p c u r -> p c r u"),
+                .rearrange("p (c r u) -> p c r u", c=PASSES, u=2)
             )
+            src = bank[:].rearrange("p c u r -> p c r u")
+            if on_vector:
+                nc.vector.tensor_copy(out=dst, in_=src)
+            else:
+                nc.scalar.copy(out=dst, in_=src)
+
+        sorted_words = {}
+        turned_words = {}
+
+        def sort_rows(name, r, on_vector=False):
+            sorted_words[name, r] = stage.tile(
+                [P, WORDS], F32, name="sorted_words", tag="sorted_words", align_bytes=64
+            )
+            dst = sorted_words[name, r][:].rearrange("p (s u i) -> p s u i", u=2, i=SQUARE)
+            src = (
+                raw[name][:]
+                .bitcast(F32)[:, r * WORDS : (r + 1) * WORDS]
+                .rearrange("p (s i u) -> p s u i", u=2, i=SQUARE)
+            )
+            if on_vector:
+                nc.vector.tensor_copy(out=dst, in_=src)
+            else:
+                nc.scalar.copy(out=dst, in_=src)
+
+        def transpose_on_vector(name, r):
+            turned_words[name, r] = stage.tile(
+                [P, WORDS], F32, name="turned_words", tag="turned_words", align_bytes=64
+            )
+            nc.vector.transpose(out=turned_words[name, r][:], in_=sorted_words[name, r][:])
+
+        def group_rows(name, r, on_vector=True):
+            grouped_in[name, r] = stage.tile(
+                [P, PASSES * P * PACK], BF16, name="grouped_in", tag="grouped_in", align_bytes=64
+            )
+            dst = (
+                grouped_in[name, r][:]
+                .bitcast(F32)
+                .rearrange("p (c g j u) -> p c g j u", c=PASSES, j=SQUARE, u=2)
+            )
+            src = turned_words[name, r][:].rearrange(
+                "p (g c u j) -> p c g j u", c=PASSES, j=SQUARE, u=2
+            )
+            for c in range(PASSES):
+                if on_vector:
+                    nc.vector.tensor_copy(out=dst[:, c], in_=src[:, c])
+                else:
+                    nc.scalar.copy(out=dst[:, c], in_=src[:, c])
 
         def quantise_rows(name, r):
             first = r * PASSES * P
@@ -127,18 +171,6 @@ def tile_attentionnet_pa_kernel(tc, x, wq, wk, out):
             )
 
         row_order = [(name, r) for name, first, count in loads for r in range(first, first + count)]
-        to_sort = row_order[UNSORTED:]
-
-        def sort_ahead(count):
-            for n in range(min(count, len(to_sort))):
-                sort_words(*to_sort.pop(0))
-
-        def transpose_chunk(name):
-            for r in range(TILES):
-                transpose_rows(name, r)
-                if r > 0:
-                    quantise_rows(name, r - 1)
-            quantise_rows(name, TILES - 1)
 
         qk_codes = {}
         qk_scales = {}
@@ -257,9 +289,9 @@ def tile_attentionnet_pa_kernel(tc, x, wq, wk, out):
             )
             nc.sync.dma_start(out=out[b, i * P : (i + 1) * P, :], in_=weights[b, i][:])
 
-        def transpose_pair(n):
-            for name, r in row_order[n : n + 2]:
-                transpose_rows(name, r)
+        def transpose_pair(n, on_vector=()):
+            for m, (name, r) in enumerate(row_order[n : n + 2]):
+                transpose_rows(name, r, m in on_vector)
 
         def quantise_pair(n):
             for name, r in row_order[n : n + 2]:
@@ -278,99 +310,119 @@ def tile_attentionnet_pa_kernel(tc, x, wq, wk, out):
         quantise_rows(*row_order[3])
         transpose_rows(*row_order[5])
         quantise_rows(*row_order[4])
-        sort_ahead(1)
         transpose_pair(6)
         quantise_rows(*row_order[5])
-        sort_ahead(1)
         multiply(*("k", 0, 0, 0), [0])
         multiply(*("k", 0, 0, 1), [0])
         multiply(*("k", 0, 0, 0), [1])
         multiply(*("k", 0, 0, 1), [1])
         quantise_pair(6)
-        sort_ahead(2)
         multiply(*("k", 0, 0, 0), [2,3])
         multiply(*("k", 0, 0, 1), [2,3])
         empty_projected([("k", 0, 0, 0), ("k", 0, 0, 1)], [])
         transpose_pair(8)
         quantise_projected([("k", 0, 0, 0), ("k", 0, 0, 1)])
-        sort_ahead(2)
         quantise_pair(8)
         multiply(*("k", 0, 0, 2), range(PACK))
         multiply(*("k", 0, 0, 3), range(PACK))
         empty_projected([("k", 0, 0, 2), ("k", 0, 0, 3)], [0])
         transpose_pair(10)
-        sort_ahead(2)
         quantise_projected([("k", 0, 0, 2), ("k", 0, 0, 3)])
         quantise_pair(10)
-        sort_ahead(2)
         transpose_pair(12)
         transpose_pair(14)
         multiply(*("k", 1, 0, 0), range(PACK))
         multiply(*("k", 1, 0, 1), range(PACK))
         empty_projected([("k", 1, 0, 0), ("k", 1, 0, 1)], [1])
         quantise_pair(12)
-        sort_ahead(2)
         quantise_pair(14)
         quantise_projected([("k", 1, 0, 0), ("k", 1, 0, 1)])
-        sort_ahead(2)
-        project([("k", 1, 0, 2), ("k", 1, 0, 3)], [])
+        multiply(*("k", 1, 0, 2), range(PACK))
+        multiply(*("k", 1, 0, 3), range(PACK))
+        empty_projected([("k", 1, 0, 2), ("k", 1, 0, 3)], [])
         transpose_pair(16)
+        quantise_projected([("k", 1, 0, 2), ("k", 1, 0, 3)])
         transpose_pair(18)
-        sort_ahead(2)
         quantise_pair(16)
         multiply(*("q", 0, 0, 0), range(PACK))
         multiply(*("q", 0, 0, 1), range(PACK))
         empty_projected([("q", 0, 0, 0), ("q", 0, 0, 1)], [1])
         quantise_pair(18)
         quantise_projected([("q", 0, 0, 0), ("q", 0, 0, 1)])
-        sort_ahead(2)
-        project([("q", 0, 0, 2), ("q", 0, 0, 3)], [])
-        transpose_pair(20)
-        transpose_pair(22)
-        quantise_pair(20)
+        sort_rows(*row_order[20])
+        transpose_on_vector(*row_order[20])
+        multiply(*("q", 0, 0, 2), range(PACK))
+        multiply(*("q", 0, 0, 3), range(PACK))
+        empty_projected([("q", 0, 0, 2), ("q", 0, 0, 3)], [])
+        group_rows(*row_order[20])
+        sort_rows(*row_order[21])
+        quantise_projected([("q", 0, 0, 2), ("q", 0, 0, 3)])
+        quantise_rows(*row_order[20])
+        transpose_on_vector(*row_order[21])
         multiply(*("q", 1, 0, 0), range(PACK))
+        multiply(*("q", 1, 0, 1), range(PACK))
+        empty_projected([("q", 1, 0, 0), ("q", 1, 0, 1)], [])
+        quantise_projected([("q", 1, 0, 0), ("q", 1, 0, 1)])
+        group_rows(*row_order[21])
+        sort_rows(*row_order[22])
+        quantise_rows(*row_order[21])
+        transpose_on_vector(*row_order[22])
+        multiply(*("q", 1, 0, 2), range(PACK))
+        multiply(*("q", 1, 0, 3), range(PACK))
+        empty_projected([("q", 1, 0, 2), ("q", 1, 0, 3)], [])
+        quantise_projected([("q", 1, 0, 2), ("q", 1, 0, 3)])
+        group_rows(*row_order[22])
+        sort_rows(*row_order[23])
+        quantise_rows(*row_order[22])
+        transpose_on_vector(*row_order[23])
         multiply(*("k", 0, 1, 0), range(PACK))
-        empty_projected([("q", 1, 0, 0), ("k", 0, 1, 0)], [1])
-        quantise_pair(22)
-        quantise_projected([("q", 1, 0, 0), ("k", 0, 1, 0)])
-        project([("q", 1, 0, 1), ("k", 0, 1, 1)], [])
+        multiply(*("k", 1, 1, 0), range(PACK))
+        empty_projected([("k", 0, 1, 0), ("k", 1, 1, 0)], [])
+        quantise_projected([("k", 0, 1, 0), ("k", 1, 1, 0)])
+        group_rows(*row_order[23])
         scores_and_shift(*tiles[0])
-        project([("q", 1, 0, 2), ("k", 0, 1, 2)], [])
+        quantise_rows(*row_order[23])
+        multiply(*("k", 0, 1, 1), range(PACK))
+        multiply(*("k", 1, 1, 1), range(PACK))
+        empty_projected([("k", 0, 1, 1), ("k", 1, 1, 1)], [])
+        quantise_projected([("k", 0, 1, 1), ("k", 1, 1, 1)])
         scores_and_shift(*tiles[1])
         exponentials(*tiles[0])
-        project([("q", 1, 0, 3), ("k", 0, 1, 3)], [])
+        multiply(*("k", 0, 1, 2), range(PACK))
+        multiply(*("k", 1, 1, 2), range(PACK))
+        empty_projected([("k", 0, 1, 2), ("k", 1, 1, 2)], [])
+        quantise_projected([("k", 0, 1, 2), ("k", 1, 1, 2)])
         scores_and_shift(*tiles[2])
         invert_sum(*tiles[0])
         exponentials(*tiles[1])
-        multiply(*("k", 1, 1, 0), range(PACK))
-        multiply(*("k", 1, 1, 1), range(PACK))
-        empty_projected([("k", 1, 1, 0), ("k", 1, 1, 1)], [])
+        multiply(*("k", 0, 1, 3), range(PACK))
+        multiply(*("k", 1, 1, 3), range(PACK))
+        empty_projected([("k", 0, 1, 3), ("k", 1, 1, 3)], [])
         normalise_and_store(*tiles[0], nc.vector)
-        quantise_projected([("k", 1, 1, 0), ("k", 1, 1, 1)])
+        quantise_projected([("k", 0, 1, 3), ("k", 1, 1, 3)])
         scores_and_shift(*tiles[3])
         invert_sum(*tiles[1])
         exponentials(*tiles[2])
-        multiply(*("k", 1, 1, 2), range(PACK))
-        multiply(*("k", 1, 1, 3), range(PACK))
-        empty_projected([("k", 1, 1, 2), ("k", 1, 1, 3)], [1])
-        normalise_and_store(*tiles[1], nc.vector)
-        quantise_projected([("k", 1, 1, 2), ("k", 1, 1, 3)])
-        invert_sum(*tiles[2])
-        exponentials(*tiles[3])
         multiply(*("q", 0, 1, 0), range(PACK))
         multiply(*("q", 1, 1, 0), range(PACK))
         empty_projected([("q", 0, 1, 0), ("q", 1, 1, 0)], [1])
-        normalise_and_store(*tiles[2], nc.vector)
+        normalise_and_store(*tiles[1], nc.vector)
         quantise_projected([("q", 0, 1, 0), ("q", 1, 1, 0)])
-        invert_sum(*tiles[3])
+        invert_sum(*tiles[2])
+        exponentials(*tiles[3])
         multiply(*("q", 0, 1, 1), range(PACK))
         multiply(*("q", 1, 1, 1), range(PACK))
         empty_projected([("q", 0, 1, 1), ("q", 1, 1, 1)], [1])
-        normalise_and_store(*tiles[3], nc.vector)
+        normalise_and_store(*tiles[2], nc.vector)
         quantise_projected([("q", 0, 1, 1), ("q", 1, 1, 1)])
-        project([("q", 0, 1, 2), ("q", 1, 1, 2)], [1])
+        invert_sum(*tiles[3])
+        multiply(*("q", 0, 1, 2), range(PACK))
+        multiply(*("q", 1, 1, 2), range(PACK))
+        empty_projected([("q", 0, 1, 2), ("q", 1, 1, 2)], [1])
+        normalise_and_store(*tiles[3], nc.vector)
+        quantise_projected([("q", 0, 1, 2), ("q", 1, 1, 2)])
         scores_and_shift(*tiles[4])
-        project([("q", 0, 1, 3), ("q", 1, 1, 3)], [1])
+        project([("q", 0, 1, 3), ("q", 1, 1, 3)], [])
         scores_and_shift(*tiles[5])
         exponentials(*tiles[4])
         scores_and_shift(*tiles[6])

@@ -20,6 +20,7 @@ PASSES = D // K_PASS
 TILES = S // P
 WORDS = D // 2
 INV_SQRT = 1.0 / math.sqrt(D // 8)
+RUN = 4
 SQUARE = 32
 
 FLOPS = 2 * (2 * B * S * D * D) + 2 * B * S * S * D
@@ -209,8 +210,8 @@ def tile_attentionnet_pa_kernel(tc, x, wq, wk, out):
                 grouped_qk[bank] = stage.tile(
                     [P, P * PACK], BF16, name="grouped_qk", tag="grouped_qk", align_bytes=64
                 )
-                dst = grouped_qk[bank][:].rearrange("p (r t) -> p r t", t=PACK)
-                src = open_banks[bank][:].rearrange("p t r -> p r t")
+                dst = grouped_qk[bank][:].rearrange("p (c i t) -> p c t i", i=RUN, t=PACK)
+                src = open_banks[bank][:].rearrange("p t (c i) -> p c t i", i=RUN)
                 if n in on_vector:
                     nc.vector.tensor_copy(out=dst, in_=src)
                 else:
@@ -278,16 +279,21 @@ def tile_attentionnet_pa_kernel(tc, x, wq, wk, out):
             inverse[b, i] = small.tile([P, 1], F32, name="inverse", tag="inverse")
             nc.vector.reciprocal(out=inverse[b, i][:], in_=row_sum[b, i][:])
 
-        def normalise_and_store(b, i, engine):
-            engine.tensor_scalar(
-                out=weights[b, i][:],
-                in0=weights[b, i][:],
-                scalar1=inverse[b, i][:],
-                scalar2=0.0,
-                op0=ALU.mult,
-                op1=ALU.add,
-            )
-            nc.sync.dma_start(out=out[b, i * P : (i + 1) * P, :], in_=weights[b, i][:])
+        def normalise_and_store(b, i, engine, parts=1):
+            width = S // parts
+            for first in range(0, S, width):
+                part = weights[b, i][:, first : first + width]
+                engine.tensor_scalar(
+                    out=part,
+                    in0=part,
+                    scalar1=inverse[b, i][:],
+                    scalar2=0.0,
+                    op0=ALU.mult,
+                    op1=ALU.add,
+                )
+                nc.sync.dma_start(
+                    out=out[b, i * P : (i + 1) * P, first : first + width], in_=part
+                )
 
         def transpose_pair(n, on_vector=()):
             for m, (name, r) in enumerate(row_order[n : n + 2]):
@@ -329,20 +335,20 @@ def tile_attentionnet_pa_kernel(tc, x, wq, wk, out):
         transpose_pair(10)
         quantise_projected([("k", 0, 0, 2), ("k", 0, 0, 3)])
         quantise_pair(10)
-        transpose_pair(12)
-        transpose_pair(14)
+        transpose_pair(12, [0])
+        transpose_pair(14, [0])
         multiply(*("k", 1, 0, 0), range(PACK))
         multiply(*("k", 1, 0, 1), range(PACK))
-        empty_projected([("k", 1, 0, 0), ("k", 1, 0, 1)], [1])
         quantise_pair(12)
+        empty_projected([("k", 1, 0, 0), ("k", 1, 0, 1)], [1])
         quantise_pair(14)
         quantise_projected([("k", 1, 0, 0), ("k", 1, 0, 1)])
         multiply(*("k", 1, 0, 2), range(PACK))
         multiply(*("k", 1, 0, 3), range(PACK))
         empty_projected([("k", 1, 0, 2), ("k", 1, 0, 3)], [])
-        transpose_pair(16)
+        transpose_pair(16, [0])
         quantise_projected([("k", 1, 0, 2), ("k", 1, 0, 3)])
-        transpose_pair(18)
+        transpose_pair(18, [0])
         quantise_pair(16)
         multiply(*("q", 0, 0, 0), range(PACK))
         multiply(*("q", 0, 0, 1), range(PACK))
@@ -418,7 +424,7 @@ def tile_attentionnet_pa_kernel(tc, x, wq, wk, out):
         invert_sum(*tiles[3])
         multiply(*("q", 0, 1, 2), range(PACK))
         multiply(*("q", 1, 1, 2), range(PACK))
-        empty_projected([("q", 0, 1, 2), ("q", 1, 1, 2)], [1])
+        empty_projected([("q", 0, 1, 2), ("q", 1, 1, 2)], [])
         normalise_and_store(*tiles[3], nc.vector)
         quantise_projected([("q", 0, 1, 2), ("q", 1, 1, 2)])
         scores_and_shift(*tiles[4])
@@ -426,15 +432,15 @@ def tile_attentionnet_pa_kernel(tc, x, wq, wk, out):
         scores_and_shift(*tiles[5])
         exponentials(*tiles[4])
         scores_and_shift(*tiles[6])
-        invert_sum(*tiles[4])
         exponentials(*tiles[5])
+        invert_sum(*tiles[4])
         scores_and_shift(*tiles[7])
         normalise_and_store(*tiles[4], nc.vector)
-        invert_sum(*tiles[5])
         exponentials(*tiles[6])
+        invert_sum(*tiles[5])
         normalise_and_store(*tiles[5], nc.vector)
-        invert_sum(*tiles[6])
         exponentials(*tiles[7])
+        invert_sum(*tiles[6])
         normalise_and_store(*tiles[6], nc.vector)
         invert_sum(*tiles[7])
-        normalise_and_store(*tiles[7], nc.vector)
+        normalise_and_store(*tiles[7], nc.vector, 2)

@@ -53,7 +53,7 @@ def tile_attentionnet_pa_kernel(tc, x, wq, wk, out):
         loads += [("k0", r, 1) for r in range(TILES)]
         loads += [("x0", 2, 1), ("x0", 3, 1)]
         loads += [(name, r, 2) for name in ("k1", "q0") for r in (0, 2)]
-        loads += [("q1", 0, TILES), ("x1", 0, TILES)]
+        loads += [("x1", 0, 2), ("q1", 0, TILES), ("x1", 2, 2)]
         sources = {
             "x0": chunk_of_tokens(0),
             "k0": chunk_of_weights(wk, 0),
@@ -73,20 +73,20 @@ def tile_attentionnet_pa_kernel(tc, x, wq, wk, out):
             in_scales[name] = keep.tile(
                 [P, TILES * PASSES * P], U8, name="scales_" + name, align_bytes=64
             )
-        def load_for_vector():
+        def load_for_vector(first_group, end_group):
             slots = raw["x1"][:].rearrange("p (g c k) -> p g c k", c=PASSES, k=P)
             tokens = x[1].rearrange("(g j) k -> j g k", j=SQUARE)
             for c in range(PASSES):
                 for a in range(P // SQUARE):
                     first = c * K_PASS + a * P
                     nc.sync.dma_start(
-                        out=slots[SQUARE * a : SQUARE * (a + 1), :, c, :],
-                        in_=tokens[:, :, first : first + P],
+                        out=slots[SQUARE * a : SQUARE * (a + 1), first_group:end_group, c, :],
+                        in_=tokens[:, first_group:end_group, first : first + P],
                     )
 
         for name, r, count in loads:
             if name == "x1":
-                load_for_vector()
+                load_for_vector(r * P // SQUARE, (r + count) * P // SQUARE)
                 continue
             rows = raw[name][:].rearrange("p (r k) -> p r k", r=TILES)
             nc.sync.dma_start(
@@ -346,87 +346,87 @@ def tile_attentionnet_pa_kernel(tc, x, wq, wk, out):
         multiply(*("k", 1, 0, 2), range(PACK))
         multiply(*("k", 1, 0, 3), range(PACK))
         empty_projected([("k", 1, 0, 2), ("k", 1, 0, 3)], [])
-        transpose_pair(16, [0])
         quantise_projected([("k", 1, 0, 2), ("k", 1, 0, 3)])
-        transpose_pair(18, [0])
-        quantise_pair(16)
+        sort_rows(*row_order[16])
         multiply(*("q", 0, 0, 0), range(PACK))
         multiply(*("q", 0, 0, 1), range(PACK))
         empty_projected([("q", 0, 0, 0), ("q", 0, 0, 1)], [1])
-        quantise_pair(18)
+        transpose_on_vector(*row_order[16])
         quantise_projected([("q", 0, 0, 0), ("q", 0, 0, 1)])
-        sort_rows(*row_order[20])
-        transpose_on_vector(*row_order[20])
+        sort_rows(*row_order[17])
+        group_rows(*row_order[16])
+        transpose_on_vector(*row_order[17])
+        quantise_rows(*row_order[16])
+        group_rows(*row_order[17])
         multiply(*("q", 0, 0, 2), range(PACK))
         multiply(*("q", 0, 0, 3), range(PACK))
         empty_projected([("q", 0, 0, 2), ("q", 0, 0, 3)], [])
-        group_rows(*row_order[20])
-        sort_rows(*row_order[21])
+        transpose_pair(18)
+        quantise_rows(*row_order[17])
         quantise_projected([("q", 0, 0, 2), ("q", 0, 0, 3)])
-        quantise_rows(*row_order[20])
-        transpose_on_vector(*row_order[21])
-        multiply(*("q", 1, 0, 0), range(PACK))
-        multiply(*("q", 1, 0, 1), range(PACK))
-        empty_projected([("q", 1, 0, 0), ("q", 1, 0, 1)], [])
-        quantise_projected([("q", 1, 0, 0), ("q", 1, 0, 1)])
-        group_rows(*row_order[21])
-        sort_rows(*row_order[22])
-        quantise_rows(*row_order[21])
-        transpose_on_vector(*row_order[22])
-        multiply(*("q", 1, 0, 2), range(PACK))
-        multiply(*("q", 1, 0, 3), range(PACK))
-        empty_projected([("q", 1, 0, 2), ("q", 1, 0, 3)], [])
-        quantise_projected([("q", 1, 0, 2), ("q", 1, 0, 3)])
-        group_rows(*row_order[22])
-        sort_rows(*row_order[23])
-        quantise_rows(*row_order[22])
-        transpose_on_vector(*row_order[23])
+        transpose_pair(20, [0])
+        quantise_pair(18)
         multiply(*("k", 0, 1, 0), range(PACK))
         multiply(*("k", 1, 1, 0), range(PACK))
         empty_projected([("k", 0, 1, 0), ("k", 1, 1, 0)], [])
+        quantise_pair(20)
         quantise_projected([("k", 0, 1, 0), ("k", 1, 1, 0)])
-        group_rows(*row_order[23])
-        scores_and_shift(*tiles[0])
-        quantise_rows(*row_order[23])
+        sort_rows(*row_order[22])
         multiply(*("k", 0, 1, 1), range(PACK))
         multiply(*("k", 1, 1, 1), range(PACK))
         empty_projected([("k", 0, 1, 1), ("k", 1, 1, 1)], [])
+        transpose_on_vector(*row_order[22])
         quantise_projected([("k", 0, 1, 1), ("k", 1, 1, 1)])
-        scores_and_shift(*tiles[1])
-        exponentials(*tiles[0])
+        sort_rows(*row_order[23])
+        group_rows(*row_order[22])
+        multiply(*("q", 1, 0, 0), range(PACK))
+        multiply(*("q", 1, 0, 1), range(PACK))
+        empty_projected([("q", 1, 0, 0), ("q", 1, 0, 1)], [])
+        transpose_on_vector(*row_order[23])
+        quantise_rows(*row_order[22])
+        quantise_projected([("q", 1, 0, 0), ("q", 1, 0, 1)])
+        group_rows(*row_order[23])
+        multiply(*("q", 1, 0, 2), range(PACK))
+        multiply(*("q", 1, 0, 3), range(PACK))
+        empty_projected([("q", 1, 0, 2), ("q", 1, 0, 3)], [])
+        quantise_rows(*row_order[23])
+        quantise_projected([("q", 1, 0, 2), ("q", 1, 0, 3)])
+        scores_and_shift(*tiles[0])
         multiply(*("k", 0, 1, 2), range(PACK))
         multiply(*("k", 1, 1, 2), range(PACK))
         empty_projected([("k", 0, 1, 2), ("k", 1, 1, 2)], [])
         quantise_projected([("k", 0, 1, 2), ("k", 1, 1, 2)])
-        scores_and_shift(*tiles[2])
-        invert_sum(*tiles[0])
-        exponentials(*tiles[1])
+        scores_and_shift(*tiles[1])
+        exponentials(*tiles[0])
         multiply(*("k", 0, 1, 3), range(PACK))
         multiply(*("k", 1, 1, 3), range(PACK))
         empty_projected([("k", 0, 1, 3), ("k", 1, 1, 3)], [])
-        normalise_and_store(*tiles[0], nc.vector)
         quantise_projected([("k", 0, 1, 3), ("k", 1, 1, 3)])
+        scores_and_shift(*tiles[2])
+        invert_sum(*tiles[0])
+        exponentials(*tiles[1])
+        multiply(*("q", 0, 1, 0), range(PACK))
+        multiply(*("q", 1, 1, 0), range(PACK))
+        empty_projected([("q", 0, 1, 0), ("q", 1, 1, 0)], [])
+        normalise_and_store(*tiles[0], nc.vector)
+        quantise_projected([("q", 0, 1, 0), ("q", 1, 1, 0)])
         scores_and_shift(*tiles[3])
         invert_sum(*tiles[1])
         exponentials(*tiles[2])
-        multiply(*("q", 0, 1, 0), range(PACK))
-        multiply(*("q", 1, 1, 0), range(PACK))
-        empty_projected([("q", 0, 1, 0), ("q", 1, 1, 0)], [1])
-        normalise_and_store(*tiles[1], nc.vector)
-        quantise_projected([("q", 0, 1, 0), ("q", 1, 1, 0)])
-        invert_sum(*tiles[2])
-        exponentials(*tiles[3])
         multiply(*("q", 0, 1, 1), range(PACK))
         multiply(*("q", 1, 1, 1), range(PACK))
         empty_projected([("q", 0, 1, 1), ("q", 1, 1, 1)], [1])
-        normalise_and_store(*tiles[2], nc.vector)
+        normalise_and_store(*tiles[1], nc.vector)
         quantise_projected([("q", 0, 1, 1), ("q", 1, 1, 1)])
-        invert_sum(*tiles[3])
+        invert_sum(*tiles[2])
+        exponentials(*tiles[3])
         multiply(*("q", 0, 1, 2), range(PACK))
         multiply(*("q", 1, 1, 2), range(PACK))
         empty_projected([("q", 0, 1, 2), ("q", 1, 1, 2)], [])
-        normalise_and_store(*tiles[3], nc.vector)
+        normalise_and_store(*tiles[2], nc.vector)
+        invert_sum(*tiles[3])
         quantise_projected([("q", 0, 1, 2), ("q", 1, 1, 2)])
+        normalise_and_store(*tiles[3], nc.vector)
         scores_and_shift(*tiles[4])
         project([("q", 0, 1, 3), ("q", 1, 1, 3)], [])
         scores_and_shift(*tiles[5])
@@ -435,11 +435,11 @@ def tile_attentionnet_pa_kernel(tc, x, wq, wk, out):
         exponentials(*tiles[5])
         invert_sum(*tiles[4])
         scores_and_shift(*tiles[7])
-        normalise_and_store(*tiles[4], nc.vector)
         exponentials(*tiles[6])
         invert_sum(*tiles[5])
-        normalise_and_store(*tiles[5], nc.vector)
+        normalise_and_store(*tiles[4], nc.vector)
         exponentials(*tiles[7])
+        normalise_and_store(*tiles[5], nc.vector)
         invert_sum(*tiles[6])
         normalise_and_store(*tiles[6], nc.vector)
         invert_sum(*tiles[7])

@@ -49,9 +49,7 @@ def tile_attentionnet_pa_kernel(tc, x, wq, wk, out):
         def chunk_of_tokens(b):
             return x[b].rearrange("(i p) k -> p i k", p=P)
 
-        loads = [("x0", 0, 1), ("x0", 1, 1)]
-        loads += [("k0", r, 1) for r in range(TILES)]
-        loads += [("x0", 2, 1), ("x0", 3, 1)]
+        loads = [(name, r, 1) for name in ("x0", "k0") for r in range(TILES)]
         loads += [(name, r, 2) for name in ("k1", "q0") for r in (0, 2)]
         loads += [("x1", 0, 2), ("q1", 0, TILES), ("x1", 2, 2)]
         sources = {
@@ -68,10 +66,10 @@ def tile_attentionnet_pa_kernel(tc, x, wq, wk, out):
         for name in sources:
             raw[name] = keep.tile([P, TILES * D], BF16, name="raw_" + name)
             in_codes[name] = keep.tile(
-                [P, TILES * PASSES * P], U32, name="codes_" + name, align_bytes=64
+                [P, TILES * PASSES * P], U32, name="codes_" + name, align_bytes=256
             )
             in_scales[name] = keep.tile(
-                [P, TILES * PASSES * P], U8, name="scales_" + name, align_bytes=64
+                [P, TILES * PASSES * P], U8, name="scales_" + name, align_bytes=256
             )
         def load_for_vector(first_group, end_group):
             slots = raw["x1"][:].rearrange("p (g c k) -> p g c k", c=PASSES, k=P)
@@ -108,7 +106,7 @@ def tile_attentionnet_pa_kernel(tc, x, wq, wk, out):
                     columns = words[:, first + u : first + 2 * P : 2]
                     nc.tensor.transpose(bank[:, c, u, :], columns, identity[:])
             grouped_in[name, r] = stage.tile(
-                [P, PASSES * P * PACK], BF16, name="grouped_in", tag="grouped_in", align_bytes=64
+                [P, PASSES * P * PACK], BF16, name="grouped_in", tag="grouped_in", align_bytes=256
             )
             dst = (
                 grouped_in[name, r][:]
@@ -126,7 +124,7 @@ def tile_attentionnet_pa_kernel(tc, x, wq, wk, out):
 
         def sort_rows(name, r, on_vector=False):
             sorted_words[name, r] = stage.tile(
-                [P, WORDS], F32, name="sorted_words", tag="sorted_words", align_bytes=64
+                [P, WORDS], F32, name="sorted_words", tag="sorted_words", align_bytes=256
             )
             dst = sorted_words[name, r][:].rearrange("p (s u i) -> p s u i", u=2, i=SQUARE)
             src = (
@@ -141,13 +139,13 @@ def tile_attentionnet_pa_kernel(tc, x, wq, wk, out):
 
         def transpose_on_vector(name, r):
             turned_words[name, r] = stage.tile(
-                [P, WORDS], F32, name="turned_words", tag="turned_words", align_bytes=64
+                [P, WORDS], F32, name="turned_words", tag="turned_words", align_bytes=256
             )
             nc.vector.transpose(out=turned_words[name, r][:], in_=sorted_words[name, r][:])
 
         def group_rows(name, r, on_vector=True):
             grouped_in[name, r] = stage.tile(
-                [P, PASSES * P * PACK], BF16, name="grouped_in", tag="grouped_in", align_bytes=64
+                [P, PASSES * P * PACK], BF16, name="grouped_in", tag="grouped_in", align_bytes=256
             )
             dst = (
                 grouped_in[name, r][:]
@@ -178,10 +176,10 @@ def tile_attentionnet_pa_kernel(tc, x, wq, wk, out):
         for name in ("q", "k"):
             for b in range(B):
                 qk_codes[name, b] = keep.tile(
-                    [P, PASSES * S], U32, name="proj_codes_%s%d" % (name, b), align_bytes=64
+                    [P, PASSES * S], U32, name="proj_codes_%s%d" % (name, b), align_bytes=256
                 )
                 qk_scales[name, b] = keep.tile(
-                    [P, PASSES * S], U8, name="proj_scales_%s%d" % (name, b), align_bytes=64
+                    [P, PASSES * S], U8, name="proj_scales_%s%d" % (name, b), align_bytes=256
                 )
 
         open_banks = {}
@@ -208,7 +206,7 @@ def tile_attentionnet_pa_kernel(tc, x, wq, wk, out):
         def empty_projected(banks, on_vector):
             for n, bank in enumerate(banks):
                 grouped_qk[bank] = stage.tile(
-                    [P, P * PACK], BF16, name="grouped_qk", tag="grouped_qk", align_bytes=64
+                    [P, P * PACK], BF16, name="grouped_qk", tag="grouped_qk", align_bytes=256
                 )
                 dst = grouped_qk[bank][:].rearrange("p (c i t) -> p c t i", i=RUN, t=PACK)
                 src = open_banks[bank][:].rearrange("p t (c i) -> p c t i", i=RUN)
@@ -320,20 +318,27 @@ def tile_attentionnet_pa_kernel(tc, x, wq, wk, out):
         quantise_rows(*row_order[5])
         multiply(*("k", 0, 0, 0), [0])
         multiply(*("k", 0, 0, 1), [0])
+        multiply(*("k", 0, 0, 2), [0])
+        multiply(*("k", 0, 0, 3), [0])
         multiply(*("k", 0, 0, 0), [1])
         multiply(*("k", 0, 0, 1), [1])
+        multiply(*("k", 0, 0, 2), [1])
+        multiply(*("k", 0, 0, 3), [1])
         quantise_pair(6)
         multiply(*("k", 0, 0, 0), [2,3])
+        empty_projected([("k", 0, 0, 0)], [])
         multiply(*("k", 0, 0, 1), [2,3])
-        empty_projected([("k", 0, 0, 0), ("k", 0, 0, 1)], [])
+        empty_projected([("k", 0, 0, 1)], [0])
+        quantise_projected([("k", 0, 0, 0)])
+        multiply(*("k", 0, 0, 2), [2,3])
+        empty_projected([("k", 0, 0, 2)], [])
+        quantise_projected([("k", 0, 0, 1)])
+        multiply(*("k", 0, 0, 3), [2,3])
+        empty_projected([("k", 0, 0, 3)], [0])
         transpose_pair(8)
-        quantise_projected([("k", 0, 0, 0), ("k", 0, 0, 1)])
-        quantise_pair(8)
-        multiply(*("k", 0, 0, 2), range(PACK))
-        multiply(*("k", 0, 0, 3), range(PACK))
-        empty_projected([("k", 0, 0, 2), ("k", 0, 0, 3)], [0])
-        transpose_pair(10)
         quantise_projected([("k", 0, 0, 2), ("k", 0, 0, 3)])
+        quantise_pair(8)
+        transpose_pair(10)
         quantise_pair(10)
         transpose_pair(12, [0])
         transpose_pair(14, [0])

from contextlib import ExitStack
import math

import concourse.mybir as mybir
from concourse.masks import make_identity

F32 = mybir.dt.float32
BF16 = mybir.dt.bfloat16
U32 = mybir.dt.uint32
U8 = mybir.dt.uint8
FP8X4 = mybir.dt.float8_e4m3fn_x4
EXP = mybir.ActivationFunctionType.Exp
ALU = mybir.AluOpType

P = 128
PACK = 4
K_PASS = P * PACK
B, S, D = 2, 512, 1024
PASSES = D // K_PASS
TILES = S // P
WORDS = D // 2
INV_SQRT = 1.0 / math.sqrt(D // 8)
RUN = 4
SQUARE = 32

FLOPS = 2 * (2 * B * S * D * D) + 2 * B * S * S * D


def tile_attentionnet_pa_kernel(tc, x, wq, wk, out):
    nc = tc.nc
    with ExitStack() as ctx:
        keep = ctx.enter_context(tc.tile_pool(name="keep", bufs=1))
        stage = ctx.enter_context(tc.tile_pool(name="stage", bufs=8))
        small = ctx.enter_context(tc.tile_pool(name="small", bufs=4))
        work = ctx.enter_context(tc.psum_pool(name="work", bufs=5))
        score_pool = ctx.enter_context(tc.psum_pool(name="score_pool", bufs=3))
        ctx.enter_context(tc.manual_schedule())

        identity = keep.tile([P, P], F32, name="identity")
        make_identity(nc, identity[:])
        zero = keep.tile([P, 1], F32, name="zero")
        one = keep.tile([P, 1], F32, name="one")
        nc.vector.memset(zero[:], 0.0)
        nc.scalar.activation(out=one[:], in_=zero[:], func=EXP)

        def chunk_of_weights(w, g):
            return w.rearrange("(g p j) k -> g p j k", p=P, j=PACK)[g]

        def chunk_of_tokens(b):
            return x[b].rearrange("(i p) k -> p i k", p=P)

        loads = [(name, r, 1) for name in ("x0", "k0") for r in range(TILES)]
        loads += [(name, r, 2) for name in ("k1", "q0") for r in (0, 2)]
        loads += [("x1", 0, 2), ("q1", 0, TILES), ("x1", 2, 2)]
        sources = {
            "x0": chunk_of_tokens(0),
            "k0": chunk_of_weights(wk, 0),
            "k1": chunk_of_weights(wk, 1),
            "q0": chunk_of_weights(wq, 0),
            "q1": chunk_of_weights(wq, 1),
            "x1": chunk_of_tokens(1),
        }
        raw = {}
        in_codes = {}
        in_scales = {}
        for name in sources:
            raw[name] = keep.tile([P, TILES * D], BF16, name="raw_" + name)
            in_codes[name] = keep.tile(
                [P, TILES * PASSES * P], U32, name="codes_" + name, align_bytes=256
            )
            in_scales[name] = keep.tile(
                [P, TILES * PASSES * P], U8, name="scales_" + name, align_bytes=256
            )
        def load_for_vector(first_group, end_group):
            slots = raw["x1"][:].rearrange("p (g c k) -> p g c k", c=PASSES, k=P)
            tokens = x[1].rearrange("(g j) k -> j g k", j=SQUARE)
            for c in range(PASSES):
                for a in range(P // SQUARE):
                    first = c * K_PASS + a * P
                    nc.sync.dma_start(
                        out=slots[SQUARE * a : SQUARE * (a + 1), first_group:end_group, c, :],
                        in_=tokens[:, first_group:end_group, first : first + P],
                    )

        for name, r, count in loads:
            if name == "x1":
                load_for_vector(r * P // SQUARE, (r + count) * P // SQUARE)
                continue
            rows = raw[name][:].rearrange("p (r k) -> p r k", r=TILES)
            nc.sync.dma_start(
                out=rows[:, r : r + count, :], in_=sources[name][:, r : r + count, :]
            )

        def block(codes_or_scales, r, c):
            first = (r * PASSES + c) * P
            return codes_or_scales[:, first : first + P]

        grouped_in = {}

        def transpose_rows(name, r, on_vector=False):
            bank = work.tile([P, PASSES, 2, P], F32, tag="work")
            words = raw[name][:].bitcast(F32)
            for c in range(PASSES):
                for u in range(2):
                    first = r * WORDS + 2 * c * P
                    columns = words[:, first + u : first + 2 * P : 2]
                    nc.tensor.transpose(bank[:, c, u, :], columns, identity[:])
            grouped_in[name, r] = stage.tile(
                [P, PASSES * P * PACK], BF16, name="grouped_in", tag="grouped_in", align_bytes=256
            )
            dst = (
                grouped_in[name, r][:]
                .bitcast(F32)
                .rearrange("p (c r u) -> p c r u", c=PASSES, u=2)
            )
            src = bank[:].rearrange("p c u r -> p c r u")
            if on_vector:
                nc.vector.tensor_copy(out=dst, in_=src)
            else:
                nc.scalar.copy(out=dst, in_=src)

        sorted_words = {}
        turned_words = {}

        def sort_rows(name, r, on_vector=False):
            sorted_words[name, r] = stage.tile(
                [P, WORDS], F32, name="sorted_words", tag="sorted_words", align_bytes=256
            )
            dst = sorted_words[name, r][:].rearrange("p (s u i) -> p s u i", u=2, i=SQUARE)
            src = (
                raw[name][:]
                .bitcast(F32)[:, r * WORDS : (r + 1) * WORDS]
                .rearrange("p (s i u) -> p s u i", u=2, i=SQUARE)
            )
            if on_vector:
                nc.vector.tensor_copy(out=dst, in_=src)
            else:
                nc.scalar.copy(out=dst, in_=src)

        def transpose_on_vector(name, r):
            turned_words[name, r] = stage.tile(
                [P, WORDS], F32, name="turned_words", tag="turned_words", align_bytes=256
            )
            nc.vector.transpose(out=turned_words[name, r][:], in_=sorted_words[name, r][:])

        def group_rows(name, r, on_vector=True):
            grouped_in[name, r] = stage.tile(
                [P, PASSES * P * PACK], BF16, name="grouped_in", tag="grouped_in", align_bytes=256
            )
            dst = (
                grouped_in[name, r][:]
                .bitcast(F32)
                .rearrange("p (c g j u) -> p c g j u", c=PASSES, j=SQUARE, u=2)
            )
            src = turned_words[name, r][:].rearrange(
                "p (g c u j) -> p c g j u", c=PASSES, j=SQUARE, u=2
            )
            for c in range(PASSES):
                if on_vector:
                    nc.vector.tensor_copy(out=dst[:, c], in_=src[:, c])
                else:
                    nc.scalar.copy(out=dst[:, c], in_=src[:, c])

        def quantise_rows(name, r):
            first = r * PASSES * P
            nc.vector.quantize_mx(
                out=in_codes[name][:, first : first + PASSES * P].bitcast(FP8X4),
                scales=in_scales[name][:, first : first + PASSES * P],
                in_=grouped_in[name, r][:],
            )

        row_order = [(name, r) for name, first, count in loads for r in range(first, first + count)]

        qk_codes = {}
        qk_scales = {}
        for name in ("q", "k"):
            for b in range(B):
                qk_codes[name, b] = keep.tile(
                    [P, PASSES * S], U32, name="proj_codes_%s%d" % (name, b), align_bytes=256
                )
                qk_scales[name, b] = keep.tile(
                    [P, PASSES * S], U8, name="proj_scales_%s%d" % (name, b), align_bytes=256
                )

        open_banks = {}

        def multiply(name, g, b, i, features):
            w = "%s%d" % (name, g)
            xb = "x%d" % b
            if features[0] == 0:
                open_banks[name, g, b, i] = work.tile([P, PACK, P], F32, name="bank", tag="work")
            for t in features:
                for c in range(PASSES):
                    nc.tensor.matmul_mx(
                        out=open_banks[name, g, b, i][:, t, :],
                        lhsT=block(in_codes[w], t, c).bitcast(FP8X4),
                        lhsT_scale=block(in_scales[w], t, c),
                        rhs=block(in_codes[xb], i, c).bitcast(FP8X4),
                        rhs_scale=block(in_scales[xb], i, c),
                        start=(c == 0),
                        stop=(c == PASSES - 1),
                    )

        grouped_qk = {}

        def empty_projected(banks, on_vector):
            for n, bank in enumerate(banks):
                grouped_qk[bank] = stage.tile(
                    [P, P * PACK], BF16, name="grouped_qk", tag="grouped_qk", align_bytes=256
                )
                dst = grouped_qk[bank][:].rearrange("p (c i t) -> p c t i", i=RUN, t=PACK)
                src = open_banks[bank][:].rearrange("p t (c i) -> p c t i", i=RUN)
                if n in on_vector:
                    nc.vector.tensor_copy(out=dst, in_=src)
                else:
                    nc.scalar.copy(out=dst, in_=src)

        def quantise_projected(banks):
            for name, g, b, i in banks:
                first = g * S + i * P
                nc.vector.quantize_mx(
                    out=qk_codes[name, b][:, first : first + P].bitcast(FP8X4),
                    scales=qk_scales[name, b][:, first : first + P],
                    in_=grouped_qk[name, g, b, i][:],
                )

        def project(banks, on_vector):
            for bank in banks:
                multiply(*bank, range(PACK))
            empty_projected(banks, on_vector)
            quantise_projected(banks)

        score = {}
        shift = {}
        weights = {}
        row_sum = {}
        inverse = {}

        def scores_and_shift(b, i):
            score[b, i] = score_pool.tile([P, S], F32, name="score", tag="score")
            for g in range(PASSES):
                first = g * S + i * P
                nc.tensor.matmul_mx(
                    out=score[b, i][:],
                    lhsT=qk_codes["q", b][:, first : first + P].bitcast(FP8X4),
                    lhsT_scale=qk_scales["q", b][:, first : first + P],
                    rhs=qk_codes["k", b][:, g * S : (g + 1) * S].bitcast(FP8X4),
                    rhs_scale=qk_scales["k", b][:, g * S : (g + 1) * S],
                    start=(g == 0),
                    stop=(g == PASSES - 1),
                )
            shift[b, i] = small.tile([P, 1], F32, name="shift", tag="shift")
            unread = stage.tile([P, S], F32, name="unread_products", tag="unread_products")
            nc.vector.tensor_scalar(
                out=unread[:],
                in0=score[b, i][:],
                scalar1=-INV_SQRT,
                scalar2=None,
                op0=ALU.mult,
                op1=ALU.min,
                accum_out=shift[b, i][:],
            )

        def exponentials(b, i):
            weights[b, i] = stage.tile([P, S], F32, name="weights", tag="weights")
            row_sum[b, i] = small.tile([P, 1], F32, name="row_sum", tag="row_sum")
            nc.scalar.activation(
                out=weights[b, i][:],
                in_=score[b, i][:],
                func=EXP,
                bias=shift[b, i][:],
                scale=INV_SQRT,
                accum_out=row_sum[b, i][:],
            )

        def invert_sum(b, i):
            inverse[b, i] = small.tile([P, 1], F32, name="inverse", tag="inverse")
            nc.vector.reciprocal(out=inverse[b, i][:], in_=row_sum[b, i][:])

        def normalise_and_store(b, i, engine, parts=1):
            width = S // parts
            for first in range(0, S, width):
                part = weights[b, i][:, first : first + width]
                engine.tensor_scalar(
                    out=part,
                    in0=part,
                    scalar1=inverse[b, i][:],
                    scalar2=0.0,
                    op0=ALU.mult,
                    op1=ALU.add,
                )
                nc.sync.dma_start(
                    out=out[b, i * P : (i + 1) * P, first : first + width], in_=part
                )

        def transpose_pair(n, on_vector=()):
            for m, (name, r) in enumerate(row_order[n : n + 2]):
                transpose_rows(name, r, m in on_vector)

        def quantise_pair(n):
            for name, r in row_order[n : n + 2]:
                quantise_rows(name, r)

        tiles = [(b, i) for b in range(B) for i in range(TILES)]

        transpose_rows(*row_order[0])
        transpose_rows(*row_order[1])
        quantise_rows(*row_order[0])
        transpose_rows(*row_order[2])
        quantise_rows(*row_order[1])
        transpose_rows(*row_order[3])
        quantise_rows(*row_order[2])
        transpose_rows(*row_order[4])
        quantise_rows(*row_order[3])
        transpose_rows(*row_order[5])
        quantise_rows(*row_order[4])
        transpose_pair(6)
        quantise_rows(*row_order[5])
        multiply(*("k", 0, 0, 0), [0])
        multiply(*("k", 0, 0, 1), [0])
        multiply(*("k", 0, 0, 2), [0])
        multiply(*("k", 0, 0, 3), [0])
        multiply(*("k", 0, 0, 0), [1])
        multiply(*("k", 0, 0, 1), [1])
        multiply(*("k", 0, 0, 2), [1])
        multiply(*("k", 0, 0, 3), [1])
        quantise_pair(6)
        multiply(*("k", 0, 0, 0), [2,3])
        empty_projected([("k", 0, 0, 0)], [])
        multiply(*("k", 0, 0, 1), [2,3])
        empty_projected([("k", 0, 0, 1)], [0])
        quantise_projected([("k", 0, 0, 0)])
        multiply(*("k", 0, 0, 2), [2,3])
        empty_projected([("k", 0, 0, 2)], [])
        quantise_projected([("k", 0, 0, 1)])
        multiply(*("k", 0, 0, 3), [2,3])
        empty_projected([("k", 0, 0, 3)], [0])
        transpose_pair(8)
        quantise_projected([("k", 0, 0, 2), ("k", 0, 0, 3)])
        quantise_pair(8)
        transpose_pair(10)
        quantise_pair(10)
        transpose_pair(12, [0])
        transpose_pair(14, [0])
        multiply(*("k", 1, 0, 0), range(PACK))
        multiply(*("k", 1, 0, 1), range(PACK))
        quantise_pair(12)
        empty_projected([("k", 1, 0, 0), ("k", 1, 0, 1)], [1])
        quantise_pair(14)
        quantise_projected([("k", 1, 0, 0), ("k", 1, 0, 1)])
        multiply(*("k", 1, 0, 2), range(PACK))
        multiply(*("k", 1, 0, 3), range(PACK))
        empty_projected([("k", 1, 0, 2), ("k", 1, 0, 3)], [])
        quantise_projected([("k", 1, 0, 2), ("k", 1, 0, 3)])
        sort_rows(*row_order[16])
        multiply(*("q", 0, 0, 0), range(PACK))
        multiply(*("q", 0, 0, 1), range(PACK))
        empty_projected([("q", 0, 0, 0), ("q", 0, 0, 1)], [1])
        transpose_on_vector(*row_order[16])
        quantise_projected([("q", 0, 0, 0), ("q", 0, 0, 1)])
        sort_rows(*row_order[17])
        group_rows(*row_order[16])
        transpose_on_vector(*row_order[17])
        quantise_rows(*row_order[16])
        group_rows(*row_order[17])
        multiply(*("q", 0, 0, 2), range(PACK))
        multiply(*("q", 0, 0, 3), range(PACK))
        empty_projected([("q", 0, 0, 2), ("q", 0, 0, 3)], [])
        transpose_pair(18)
        quantise_rows(*row_order[17])
        quantise_projected([("q", 0, 0, 2), ("q", 0, 0, 3)])
        transpose_pair(20, [0])
        quantise_pair(18)
        multiply(*("k", 0, 1, 0), range(PACK))
        multiply(*("k", 1, 1, 0), range(PACK))
        empty_projected([("k", 0, 1, 0), ("k", 1, 1, 0)], [])
        quantise_pair(20)
        quantise_projected([("k", 0, 1, 0), ("k", 1, 1, 0)])
        sort_rows(*row_order[22])
        multiply(*("k", 0, 1, 1), range(PACK))
        multiply(*("k", 1, 1, 1), range(PACK))
        empty_projected([("k", 0, 1, 1), ("k", 1, 1, 1)], [])
        transpose_on_vector(*row_order[22])
        quantise_projected([("k", 0, 1, 1), ("k", 1, 1, 1)])
        sort_rows(*row_order[23])
        group_rows(*row_order[22])
        multiply(*("q", 1, 0, 0), range(PACK))
        multiply(*("q", 1, 0, 1), range(PACK))
        empty_projected([("q", 1, 0, 0), ("q", 1, 0, 1)], [])
        transpose_on_vector(*row_order[23])
        quantise_rows(*row_order[22])
        quantise_projected([("q", 1, 0, 0), ("q", 1, 0, 1)])
        group_rows(*row_order[23])
        multiply(*("q", 1, 0, 2), range(PACK))
        multiply(*("q", 1, 0, 3), range(PACK))
        empty_projected([("q", 1, 0, 2), ("q", 1, 0, 3)], [])
        quantise_rows(*row_order[23])
        quantise_projected([("q", 1, 0, 2), ("q", 1, 0, 3)])
        scores_and_shift(*tiles[0])
        multiply(*("k", 0, 1, 2), range(PACK))
        multiply(*("k", 1, 1, 2), range(PACK))
        empty_projected([("k", 0, 1, 2), ("k", 1, 1, 2)], [])
        quantise_projected([("k", 0, 1, 2), ("k", 1, 1, 2)])
        scores_and_shift(*tiles[1])
        exponentials(*tiles[0])
        multiply(*("k", 0, 1, 3), range(PACK))
        multiply(*("k", 1, 1, 3), range(PACK))
        empty_projected([("k", 0, 1, 3), ("k", 1, 1, 3)], [])
        quantise_projected([("k", 0, 1, 3), ("k", 1, 1, 3)])
        scores_and_shift(*tiles[2])
        invert_sum(*tiles[0])
        exponentials(*tiles[1])
        multiply(*("q", 0, 1, 0), range(PACK))
        multiply(*("q", 1, 1, 0), range(PACK))
        empty_projected([("q", 0, 1, 0), ("q", 1, 1, 0)], [])
        normalise_and_store(*tiles[0], nc.vector)
        quantise_projected([("q", 0, 1, 0), ("q", 1, 1, 0)])
        scores_and_shift(*tiles[3])
        invert_sum(*tiles[1])
        exponentials(*tiles[2])
        multiply(*("q", 0, 1, 1), range(PACK))
        multiply(*("q", 1, 1, 1), range(PACK))
        empty_projected([("q", 0, 1, 1), ("q", 1, 1, 1)], [1])
        normalise_and_store(*tiles[1], nc.vector)
        quantise_projected([("q", 0, 1, 1), ("q", 1, 1, 1)])
        invert_sum(*tiles[2])
        exponentials(*tiles[3])
        multiply(*("q", 0, 1, 2), range(PACK))
        multiply(*("q", 1, 1, 2), range(PACK))
        empty_projected([("q", 0, 1, 2), ("q", 1, 1, 2)], [])
        normalise_and_store(*tiles[2], nc.vector)
        invert_sum(*tiles[3])
        quantise_projected([("q", 0, 1, 2), ("q", 1, 1, 2)])
        normalise_and_store(*tiles[3], nc.vector)
        scores_and_shift(*tiles[4])
        project([("q", 0, 1, 3), ("q", 1, 1, 3)], [])
        scores_and_shift(*tiles[5])
        exponentials(*tiles[4])
        scores_and_shift(*tiles[6])
        exponentials(*tiles[5])
        invert_sum(*tiles[4])
        scores_and_shift(*tiles[7])
        exponentials(*tiles[6])
        invert_sum(*tiles[5])
        normalise_and_store(*tiles[4], nc.vector)
        exponentials(*tiles[7])
        normalise_and_store(*tiles[5], nc.vector)
        invert_sum(*tiles[6])
        normalise_and_store(*tiles[6], nc.vector)
        invert_sum(*tiles[7])
        normalise_and_store(*tiles[7], nc.vector, 2)
